import numpy as np
import ml_dtypes


def mxq(x, axis, fmt="e4m3"):
    dtype, down = {"e4m3": (ml_dtypes.float8_e4m3fn, 7), "e5m2": (ml_dtypes.float8_e5m2, 14)}[fmt]
    v = np.moveaxis(np.asarray(x, np.float32).astype(ml_dtypes.bfloat16).astype(np.float64), axis, -1)
    blocks = v.reshape(v.shape[:-1] + (-1, 32))
    amax = np.abs(blocks).max(-1, keepdims=True)
    byte = np.maximum(np.where(amax > 0, np.frexp(amax)[1] - 1 + 127, 0) - down, 1)
    scale = np.exp2(byte - 127.0)
    codes = (blocks / scale).astype(np.float32).astype(dtype).astype(np.float64)
    return np.moveaxis((codes * scale).reshape(v.shape), -1, axis)


WIDE = False


def mx_kscale(k):
    if not WIDE:
        return np.ones(k)
    levels = np.array([10, -10, 5, -5, 0])
    if k % 512:
        return np.exp2(np.random.permutation(np.resize(levels, k // 32))).repeat(32)
    a = np.empty((k // 512, 16))
    for p in range(k // 512):
        a[p, :8] = np.random.permutation(np.resize(levels, 8))
        for g in range(8):
            far = levels[np.abs(levels - a[p, g]) >= 10]
            a[p, g + 8] = far[np.random.randint(len(far))]
    return np.exp2(a.ravel()).repeat(32)


BF16 = ml_dtypes.bfloat16


def bf(x):
    return np.asarray(x, np.float32).astype(BF16)


def f64(x):
    return np.asarray(x).astype(np.float64)


L, B, D, D0 = 512, 4, 1024, 768
EPS_BN = 1e-5
EPS_LN = 1e-5


def setup_inputs():
    n = np.random.standard_normal
    s = mx_kscale(D)
    r = n((B, L, D))
    return {"x": bf(n((L, B, D))), "res_a": bf(np.where(r > 0, r, 0.25 * r)),
            "ctx_v": bf(n((B, L, D)) * 0.25 * s), "W_v": bf(n((D, D)) * 2.0 / np.sqrt(D) / s[None, :]),
            "bn_v_g": bf(1.0 + 0.1 * n(D)), "bn_v_b": bf(0.2 * n(D)),
            "prelu_v": bf(0.25 + 0.05 * n(1)), "ln_g": bf(1.0 + 0.1 * n(D)), "ln_b": bf(0.2 * n(D))}


def core(x, res_a, ctx_v, W_v, bn_v_g, bn_v_b, prelu_v, ln_g, ln_b):
    xq = np.swapaxes(f64(x), 0, 1)
    y = mxq(f64(ctx_v), 2, "e4m3") @ mxq(f64(W_v), 1, "e4m3").T
    mean = y.mean(axis=(0, 1))
    var = y.var(axis=(0, 1))
    z = (y - mean) / np.sqrt(var + EPS_BN) * f64(bn_v_g) + f64(bn_v_b)
    res_v = np.where(z > 0, z, f64(prelu_v) * z)
    out = np.swapaxes(xq + f64(res_a) + res_v, 0, 1)
    mu = out.mean(axis=-1, keepdims=True)
    v = out.var(axis=-1, keepdims=True)
    return (out - mu) / np.sqrt(v + EPS_LN) * f64(ln_g) + f64(ln_b)


def e4m3fn_bytes(y):
    return np.clip(np.asarray(y, np.float64), -448.0, 448.0).astype(np.float32).astype(ml_dtypes.float8_e4m3fn).view(np.uint8)


def reference(x, res_a, ctx_v, W_v, bn_v_g, bn_v_b, prelu_v, ln_g, ln_b):
    out = core(x, res_a, ctx_v, W_v, bn_v_g, bn_v_b, prelu_v, ln_g, ln_b)
    s = np.max(np.abs(out), axis=-1, keepdims=True) / 448.0
    return out, e4m3fn_bytes(out / s)

@@ -1,0 +1,462 @@
+from contextlib import ExitStack
+
+import concourse.mybir as mybir
+from concourse.masks import make_identity
+
+L, B, D = 512, 4, 1024
+EPS_BN = 1e-5
+EPS_LN = 1e-5
+FLOPS = 2 * L * B * D * D
+
+F32 = mybir.dt.float32
+BF16 = mybir.dt.bfloat16
+U32 = mybir.dt.uint32
+U8 = mybir.dt.uint8
+FP8X4 = mybir.dt.float8_e4m3fn_x4
+FP8 = mybir.dt.float8_e4m3fn
+ALU = mybir.AluOpType
+ACT = mybir.ActivationFunctionType
+AX = mybir.AxisListType
+
+P = 128
+NCT = D // P
+HC = NCT // 2
+HW = HC * P
+NCH = L // P
+CHUNK = B * P
+NPASS = D // 512
+MANUAL = True
+ON_GPSIMD = ((0, 0), (0, 1))
+NGS = (3, 3, 3, 3)
+KV = 0
+
+
+def tile_coattention_pb_kernel(
+    tc, x, res_a, ctx_v, W_v, bn_v_g, bn_v_b, prelu_v, ln_g, ln_b, out_0, out_1
+):
+    nc = tc.nc
+    with ExitStack() as ctx:
+        if MANUAL:
+            ctx.enter_context(tc.manual_schedule())
+        keep = ctx.enter_context(tc.tile_pool(name="keep", bufs=1))
+        xin = ctx.enter_context(tc.tile_pool(name="xin", bufs=4))
+        gbpsum = ctx.enter_context(tc.psum_pool(name="gbpsum", bufs=1))
+        ypool = []
+
+        ident = keep.tile([P, P], F32, name="ident")
+        make_identity(nc, ident[:])
+        one = keep.tile([P, 1], F32, name="one")
+        nc.vector.memset(one[:], 1.0)
+        zero = keep.tile([P, 1], F32, name="zero")
+        nc.vector.memset(zero[:], 0.0)
+        warm = keep.tile([P, 1], F32, name="warm")
+        nc.scalar.activation(out=warm[:], in_=one[:], func=ACT.Sqrt)
+
+        w_codes = keep.tile([P, NPASS, D], U32, name="w_codes", align_bytes=64)
+        w_scales = keep.tile([P, NPASS, D], U8, name="w_scales", align_bytes=64)
+        c_codes = keep.tile([P, NPASS, NCH * CHUNK], U32, name="c_codes", align_bytes=64)
+        c_scales = keep.tile([P, NPASS, NCH * CHUNK], U8, name="c_scales", align_bytes=64)
+        bnst = keep.tile([P, NCT, NCH, 6], F32, name="bnst")
+        ysave = keep.tile([P, HC, NCH * CHUNK], F32, name="ysave")
+        o_t = [[keep.tile([P, D], F32, name="o_%d_%d" % (r, b)) for b in range(B)] for r in range(NCH)]
+        g_sb = keep.tile([P, D], BF16, name="g_sb")
+        ident_bf = keep.tile([P, P], BF16, name="ident_bf")
+        sI_bf = keep.tile([P, P], BF16, name="sI_bf")
+        lnT_bf = keep.tile([P, 2 * NCT], BF16, name="lnT_bf")
+        a_bf = keep.tile([P, 1], BF16, name="a_bf")
+        prm_bf = keep.tile([P, P], BF16, name="prm_bf")
+        prm_f = keep.tile([P, P], F32, name="prm_f")
+        gbT = keep.tile([P, 2 * NCT], F32, name="gbT")
+        sums = keep.tile([P, NCH, B, 2], F32, name="sums")
+        a_f = keep.tile([P, 1], F32, name="a_f")
+        sig = keep.tile([P, 1], F32, name="sig")
+        k1 = keep.tile([P, 1], F32, name="k1")
+        k2 = keep.tile([P, 1], F32, name="k2")
+        mv = keep.tile([P, NCT, 2], F32, name="mv")
+        g_ps = gbpsum.tile([P, D], BF16, name="g_ps")
+        b_ps = gbpsum.tile([P, D], BF16, name="b_ps")
+
+        def mm(r, c):
+            y = ypool[-1].tile([P, CHUNK], F32, name="y")
+            for g in range(NPASS):
+                nc.tensor.matmul_mx(
+                    out=y[:],
+                    lhsT=w_codes[:, g, c * P : (c + 1) * P].bitcast(FP8X4),
+                    lhsT_scale=w_scales[:, g, c * P : (c + 1) * P],
+                    rhs=c_codes[:, g, r * CHUNK : (r + 1) * CHUNK].bitcast(FP8X4),
+                    rhs_scale=c_scales[:, g, r * CHUNK : (r + 1) * CHUNK],
+                    start=(g == 0),
+                    stop=(g == NPASS - 1),
+                )
+            return y
+
+        x_raw = {}
+        ra_raw = {}
+
+        def load_xr(r, h):
+            cols = slice(h * HW, (h + 1) * HW)
+            x_raw[r, h] = xin.tile([P, B, HW], BF16, name="x_raw")
+            nc.sync.dma_start(out=x_raw[r, h][:], in_=x[r * P : (r + 1) * P, :, cols])
+            ra_raw[r, h] = xin.tile([P, B, HW], BF16, name="ra_raw")
+            nc.sync.dma_start(
+                out=ra_raw[r, h][:], in_=res_a[:, r * P : (r + 1) * P, cols].rearrange("b l d -> l b d")
+            )
+
+        def add_xr(r, h):
+            for b in range(B):
+                nc.gpsimd.tensor_tensor(
+                    out=o_t[r][b][:, h * HW : (h + 1) * HW], in0=x_raw[r, h][:, b, :], in1=ra_raw[r, h][:, b, :],
+                    op=ALU.add,
+                )
+
+        nc.vector.memset(prm_bf[:], 0.0)
+        nc.sync.dma_start(out=prm_bf[0:NCT, :], in_=bn_v_g.rearrange("(c p) -> c p", p=P))
+        nc.sync.dma_start(out=prm_bf[NCT : 2 * NCT, :], in_=bn_v_b.rearrange("(c p) -> c p", p=P))
+        nc.sync.dma_start(out=prm_bf[2 * NCT : 3 * NCT, :], in_=ln_g.rearrange("(c p) -> c p", p=P))
+        nc.sync.dma_start(out=prm_bf[3 * NCT : 4 * NCT, :], in_=ln_b.rearrange("(c p) -> c p", p=P))
+        nc.sync.dma_start(out=a_bf[:], in_=prelu_v.partition_broadcast(P))
+        with tc.tile_pool(name="wstage", bufs=1) as wstage, tc.tile_pool(name="cstage", bufs=2) as cstage, tc.psum_pool(
+            name="tpsum", bufs=2
+        ) as tpsum, tc.psum_pool(name="ypre", bufs=4) as ypre:
+            ypool.append(ypre)
+            w_raw = {}
+            c_raw = {}
+
+            def load_w(h):
+                w_raw[h] = wstage.tile([P, HC, D], BF16, name="w_raw", bufs=2)
+                for q in range(2):
+                    nc.sync.dma_start(
+                        out=w_raw[h][:, 2 * q : 2 * q + 2, :],
+                        in_=W_v[(h * HC + 2 * q) * P : (h * HC + 2 * q + 2) * P, :].rearrange("(c p) k -> p c k", p=P),
+                    )
+
+            def load_ctx(r):
+                c_raw[r] = cstage.tile([P, B, D], BF16, name="c_raw", bufs=NCH)
+                nc.sync.dma_start(
+                    out=c_raw[r][:], in_=ctx_v[:, r * P : (r + 1) * P, :].rearrange("b l d -> l b d")
+                )
+
+            def turn(rows, grouped, on_vector):
+                words = rows.bitcast(F32)
+                tp = tpsum.tile([P, NPASS, 2, P], F32, name="tp")
+                for g in range(NPASS):
+                    for u in range(2):
+                        nc.tensor.transpose(tp[:, g, u, :], words[:, 256 * g + u : 256 * (g + 1) : 2], ident[:])
+                if on_vector:
+                    nc.vector.tensor_copy(out=grouped.bitcast(F32), in_=tp[:].rearrange("p g u r -> p g r u"))
+                else:
+                    nc.scalar.copy(out=grouped.bitcast(F32), in_=tp[:].rearrange("p g u r -> p g r u"))
+
+            def prep_w(h):
+                w_grp = wstage.tile([P, NPASS, HW, 4], BF16, name="w_grp", align_bytes=64)
+                for cc in range(HC):
+                    turn(w_raw[h][:, cc, :], w_grp[:, :, cc * P : (cc + 1) * P, :], h == 0 and cc % 2 == 0)
+                cols = slice(h * HW, (h + 1) * HW)
+                for g in range(NPASS):
+                    nc.vector.quantize_mx(
+                        out=w_codes[:, g, cols].bitcast(FP8X4),
+                        scales=w_scales[:, g, cols],
+                        in_=w_grp[:, g, :, :].rearrange("p c t -> p (c t)"),
+                    )
+
+            c_grp = {}
+
+            def turn_ctx(r):
+                c_grp[r] = cstage.tile([P, NPASS, CHUNK, 4], BF16, name="c_grp", align_bytes=64)
+                for b in range(B):
+                    turn(c_raw[r][:, b, :], c_grp[r][:, :, b * P : (b + 1) * P, :], False)
+
+            def quant_ctx(r):
+                cols = slice(r * CHUNK, (r + 1) * CHUNK)
+                for g in range(NPASS):
+                    nc.vector.quantize_mx(
+                        out=c_codes[:, g, cols].bitcast(FP8X4),
+                        scales=c_scales[:, g, cols],
+                        in_=c_grp[r][:, g, :, :].rearrange("p c t -> p (c t)"),
+                    )
+
+            def aggr(c):
+                nc.vector.bn_aggr(out=mv[:, c, :], in_=bnst[:, c, :, :].rearrange("p r s -> p (r s)"))
+
+            def mm_stats(r):
+                for c in range(NCT):
+                    y = mm(r, c)
+                    nc.vector.bn_stats(out=bnst[:, c, r, :], in_=y[:])
+                    if c < HC:
+                        nc.scalar.copy(out=ysave[:, c, r * CHUNK : (r + 1) * CHUNK], in_=y[:])
+                    if c == HC - 1 and r + 1 < NCH:
+                        quant_ctx(r + 1)
+                    if r == NCH - 1 and c > 0:
+                        aggr(c - 1)
+
+            load_w(0)
+            load_ctx(0)
+            nc.vector.tensor_copy(out=ident_bf[:], in_=ident[:])
+            nc.vector.tensor_copy(out=prm_f[:], in_=prm_bf[:])
+            prmT = tpsum.tile([P, NPASS, 2, P], F32, name="tp")
+            nc.tensor.transpose(prmT[:, 0, 0, :], prm_f[:], ident[:])
+            nc.vector.tensor_copy(out=lnT_bf[:], in_=prmT[:, 0, 0, 2 * NCT : 4 * NCT])
+            nc.vector.tensor_copy(out=gbT[:], in_=prmT[:, 0, 0, 0 : 2 * NCT])
+            for c in range(NCT):
+                nc.tensor.transpose(g_ps[:, c * P : (c + 1) * P], lnT_bf[:, c : c + 1].to_broadcast([P, P]), ident_bf[:])
+                nc.tensor.transpose(
+                    b_ps[:, c * P : (c + 1) * P], lnT_bf[:, NCT + c : NCT + c + 1].to_broadcast([P, P]), ident_bf[:]
+                )
+            nc.scalar.copy(out=g_sb[:], in_=g_ps[:])
+            load_w(1)
+            for r in range(1, NCH):
+                load_ctx(r)
+            prep_w(0)
+            load_xr(0, 0)
+            load_xr(0, 1)
+            load_xr(1, 0)
+            load_xr(1, 1)
+            turn_ctx(0)
+            quant_ctx(0)
+            prep_w(1)
+            nc.vector.tensor_copy(out=a_f[:], in_=a_bf[:])
+            nc.vector.tensor_scalar(out=sig[:], in0=a_f[:], scalar1=1.0, scalar2=-2.0, op0=ALU.is_gt, op1=ALU.mult)
+            nc.vector.tensor_scalar(out=sig[:], in0=sig[:], scalar1=1.0, scalar2=None, op0=ALU.add)
+            nc.vector.tensor_scalar(out=k1[:], in0=a_f[:], scalar1=1.0, scalar2=None, op0=ALU.min)
+            nc.vector.tensor_tensor(out=k1[:], in0=k1[:], in1=sig[:], op=ALU.mult)
+            nc.vector.tensor_scalar(out=k2[:], in0=a_f[:], scalar1=-1.0, scalar2=1.0, op0=ALU.mult, op1=ALU.add)
+            nc.vector.tensor_scalar(out=sI_bf[:], in0=ident[:], scalar1=sig[:, 0:1], scalar2=None, op0=ALU.mult)
+            for r in range(NCH):
+                if r + 1 < NCH:
+                    turn_ctx(r + 1)
+                mm_stats(r)
+            aggr(NCT - 1)
+            for rh in ON_GPSIMD:
+                add_xr(rh[0], rh[1])
+
+        bstd = keep.tile([P, NCT], F32, name="bstd")
+        nc.scalar.activation(out=bstd[:], in_=mv[:, :, 1], func=ACT.Sqrt, bias=EPS_BN, scale=1.0)
+        HALVES = (0, 1)
+        brstd = [keep.tile([P, HC], F32, name="brstd%d" % h) for h in HALVES]
+        st = [keep.tile([P, 2, HC], F32, name="st%d" % h) for h in HALVES]
+        ms = [keep.tile([P, HC], F32, name="ms%d" % h) for h in HALVES]
+        p1 = [keep.tile([P, 2, HC], F32, name="p1_%d" % h) for h in HALVES]
+        p2 = [keep.tile([P, 2, HC], F32, name="p2_%d" % h) for h in HALVES]
+        for h in HALVES:
+            nc.vector.reciprocal(out=brstd[h][:], in_=bstd[:, h * HC : (h + 1) * HC])
+        for h in HALVES:
+            nc.vector.tensor_tensor(out=st[h][:, 0, :], in0=gbT[:, h * HC : (h + 1) * HC], in1=brstd[h][:], op=ALU.mult)
+        for h in HALVES:
+            nc.vector.tensor_tensor(out=ms[h][:], in0=mv[:, h * HC : (h + 1) * HC, 0], in1=st[h][:, 0, :], op=ALU.mult)
+        for h in HALVES:
+            nc.vector.tensor_tensor(
+                out=st[h][:, 1, :], in0=gbT[:, NCT + h * HC : NCT + (h + 1) * HC], in1=ms[h][:], op=ALU.subtract
+            )
+        for h in HALVES:
+            nc.vector.tensor_scalar(out=p2[h][:], in0=st[h][:], scalar1=k2[:, 0:1], scalar2=None, op0=ALU.mult)
+        for h in HALVES:
+            nc.vector.tensor_scalar(out=p1[h][:], in0=st[h][:], scalar1=k1[:, 0:1], scalar2=None, op0=ALU.mult)
+
+        work = ctx.enter_context(tc.tile_pool(name="work", bufs=2))
+        opsum = ctx.enter_context(tc.psum_pool(name="opsum", bufs=3))
+        ypool.append(ctx.enter_context(tc.psum_pool(name="ypost", bufs=3)))
+        s12 = {}
+        ysrc = {}
+        negmu = {}
+        stdv = {}
+        t1 = {}
+        lnt = {}
+
+        def mm_f(r, ccs):
+            for cc in ccs:
+                ysrc[r, cc] = mm(r, HC + cc)
+
+        def src_of(r, h, cc):
+            return ysave[:, cc, r * CHUNK : (r + 1) * CHUNK] if h == 0 else ysrc[r, cc][:]
+
+        def new_block(r, h):
+            s12[r, h] = work.tile([P, 2, HC, CHUNK], F32, name="s12")
+
+        def s1(r, h, cc, eng):
+            if eng == "S":
+                nc.scalar.activation(
+                    out=s12[r, h][:, 0, cc, :], in_=src_of(r, h, cc), func=ACT.Identity,
+                    scale=p1[h][:, 0, cc : cc + 1], bias=p1[h][:, 1, cc : cc + 1],
+                )
+            else:
+                (nc.vector if eng == "V" else nc.gpsimd).tensor_scalar(
+                    out=s12[r, h][:, 0, cc, :], in0=src_of(r, h, cc),
+                    scalar1=p1[h][:, 0, cc : cc + 1], scalar2=p1[h][:, 1, cc : cc + 1], op0=ALU.mult, op1=ALU.add,
+                )
+
+        def s2(r, h, cc):
+            nc.scalar.activation(
+                out=s12[r, h][:, 1, cc, :], in_=src_of(r, h, cc), func=ACT.Relu,
+                scale=p2[h][:, 0, cc : cc + 1], bias=p2[h][:, 1, cc : cc + 1],
+            )
+
+        def act0(r):
+            new_block(r, 0)
+            for cc in range(HC):
+                s1(r, 0, cc, "G")
+                s2(r, 0, cc)
+
+        def act1(r, ccs):
+            for cc in ccs:
+                s2(r, 1, cc)
+                s1(r, 1, cc, "V" if cc < KV else "S")
+
+        ots = {}
+
+        def tr(r, h, bs):
+            on_pe = (r, h) not in ON_GPSIMD
+            for b in bs:
+                ot = opsum.tile([P, HW], F32, name="ot")
+                if on_pe:
+                    nc.tensor.matmul(out=ot[:], lhsT=sI_bf[:], rhs=ra_raw[r, h][:, b, :], start=True, stop=False)
+                for cc in range(HC):
+                    for j in range(2):
+                        nc.tensor.matmul(
+                            out=ot[:, cc * P : (cc + 1) * P],
+                            lhsT=s12[r, h][:, j, cc, b * P : (b + 1) * P],
+                            rhs=ident[:],
+                            is_transpose=True,
+                            start=(j == 0 and not on_pe),
+                            stop=(j == 1 and (cc == HC - 1 or not on_pe)),
+                        )
+                ots[r, h, b] = ot
+
+        def ev(r, h, bs):
+            on_pe = (r, h) not in ON_GPSIMD
+            for b in bs:
+                dst = o_t[r][b][:, h * HW : (h + 1) * HW]
+                nc.vector.scalar_tensor_tensor(
+                    out=dst, in0=ots[r, h, b][:], scalar=sig[:, 0:1], in1=(x_raw[r, h][:, b, :] if on_pe else dst),
+                    op0=ALU.mult, op1=ALU.add, accum_out=sums[:, r, b, h : h + 1],
+                )
+
+        tots = {}
+
+        def total(r):
+            tots[r] = work.tile([P, B], F32, name="tot")
+            nc.vector.tensor_reduce(out=tots[r][:], in_=sums[:, r, :, :], axis=AX.X, op=ALU.add)
+
+        def stats(r):
+            negmu[r] = work.tile([P, B], F32, name="negmu")
+            nc.scalar.activation(out=negmu[r][:], in_=tots[r][:], func=ACT.Copy, scale=-1.0 / D)
+            ssq = work.tile([P, B], F32, name="ssq")
+            for b in range(B):
+                junk = work.tile([P, D], BF16, name="junk", bufs=1)
+                nc.scalar.activation(
+                    out=junk[:], in_=o_t[r][b][:], func=ACT.Square,
+                    bias=negmu[r][:, b : b + 1], scale=1.0, accum_out=ssq[:, b : b + 1],
+                )
+            stdv[r] = work.tile([P, B], F32, name="stdv")
+            nc.scalar.activation(out=stdv[r][:], in_=ssq[:], func=ACT.Sqrt, bias=EPS_LN, scale=1.0 / D)
+
+        def stt1_g(r):
+            for b in range(B - NGS[r], B):
+                t1[r, b] = work.tile([P, D], F32, name="t1g", bufs=6)
+                nc.gpsimd.tensor_scalar(
+                    out=t1[r, b][:], in0=o_t[r][b][:], scalar1=negmu[r][:, b : b + 1], scalar2=1.0,
+                    op0=ALU.add, op1=ALU.mult,
+                )
+                nc.gpsimd.tensor_tensor(out=t1[r, b][:], in0=t1[r, b][:], in1=g_sb[:], op=ALU.mult)
+
+        def stt1_v(r):
+            for b in range(B - NGS[r]):
+                t1[r, b] = work.tile([P, D], F32, name="t1v", bufs=2)
+                nc.vector.scalar_tensor_tensor(
+                    out=t1[r, b][:], in0=o_t[r][b][:], scalar=negmu[r][:, b : b + 1], in1=g_ps[:],
+                    op0=ALU.add, op1=ALU.mult,
+                )
+
+        def ln_open(r):
+            lnt[r] = [work.tile([P, B], F32, name=n) for n in ("rstd", "amax", "ram", "r448")]
+            nc.vector.reciprocal(out=lnt[r][0][:], in_=stdv[r][:])
+
+        def stt2(r, b):
+            nc.vector.scalar_tensor_tensor(
+                out=o_t[r][b][:], in0=t1[r, b][:], scalar=lnt[r][0][:, b : b + 1], in1=b_ps[:],
+                op0=ALU.mult, op1=ALU.add,
+            )
+            nc.sync.dma_start(out=out_0[r * P : (r + 1) * P, b, :], in_=o_t[r][b][:])
+
+        def amx(r, b):
+            nc.vector.tensor_reduce(
+                out=lnt[r][1][:, b : b + 1], in_=o_t[r][b][:], axis=AX.X, op=ALU.max, apply_absolute_value=True
+            )
+
+        def rec(r, q):
+            nc.vector.reciprocal(out=lnt[r][2][:, 2 * q : 2 * q + 2], in_=lnt[r][1][:, 2 * q : 2 * q + 2])
+
+        def casts(r, q):
+            nc.scalar.activation(
+                out=lnt[r][3][:, 2 * q : 2 * q + 2], in_=lnt[r][2][:, 2 * q : 2 * q + 2], func=ACT.Copy, scale=448.0
+            )
+            for b in (2 * q, 2 * q + 1):
+                f8 = work.tile([P, D], FP8, name="f8", bufs=4)
+                if r == NCH - 1 and b == B - 1:
+                    nc.vector.tensor_scalar(
+                        out=f8[:], in0=o_t[r][b][:], scalar1=lnt[r][3][:, b : b + 1], scalar2=None, op0=ALU.mult,
+                        saturate=False,
+                    )
+                else:
+                    nc.scalar.activation(
+                        out=f8[:], in_=o_t[r][b][:], func=ACT.Identity,
+                        scale=lnt[r][3][:, b : b + 1], bias=zero[:, 0:1], saturate=False,
+                    )
+                nc.sync.dma_start(out=out_1[r * P : (r + 1) * P, b, :], in_=f8[:].bitcast(U8))
+
+        def ln_half(r, q):
+            stt2(r, 2 * q)
+            stt2(r, 2 * q + 1)
+            amx(r, 2 * q)
+            amx(r, 2 * q + 1)
+
+        def has(r):
+            return 0 <= r < NCH
+
+        for i in range(-2, NCH):
+            if has(i + 1):
+                new_block(i + 1, 1)
+                act1(i + 1, (0,))
+            if has(i):
+                stt1_v(i)
+            if has(i - 1):
+                rec(i - 1, 1)
+            if has(i + 1):
+                ev(i + 1, 0, (0,))
+                tr(i + 1, 0, (3,))
+                mm_f(i + 1, (3,))
+                act1(i + 1, (1, 2, 3))
+                ev(i + 1, 0, (1, 2))
+            if has(i):
+                ln_open(i)
+            if has(i + 1):
+                ev(i + 1, 0, (3,))
+            if has(i - 1):
+                casts(i - 1, 1)
+            if has(i):
+                ln_half(i, 0)
+            if has(i + 1):
+                tr(i + 1, 1, (0, 1, 2))
+                ev(i + 1, 1, (0,))
+            if has(i):
+                rec(i, 0)
+            if has(i + 1):
+                tr(i + 1, 1, (3,))
+                ev(i + 1, 1, (1, 2, 3))
+                total(i + 1)
+                if has(i + 3):
+                    load_xr(i + 3, 0)
+                    load_xr(i + 3, 1)
+            if has(i + 2):
+                act0(i + 2)
+            if has(i):
+                casts(i, 0)
+            if has(i + 1):
+                stats(i + 1)
+                stt1_g(i + 1)
+            if has(i + 2):
+                mm_f(i + 2, (0, 1, 2))
+                tr(i + 2, 0, (0, 1, 2))
+            if has(i):
+                ln_half(i, 1)
+        rec(NCH - 1, 1)
+        casts(NCH - 1, 1)

@@ -36,11 +36,8 @@ def tile_coattention_pb_kernel(
 ):
     nc = tc.nc
     with ExitStack() as ctx:
-        if MANUAL:
-            ctx.enter_context(tc.manual_schedule())
         keep = ctx.enter_context(tc.tile_pool(name="keep", bufs=1))
         xin = ctx.enter_context(tc.tile_pool(name="xin", bufs=4))
-        gbpsum = ctx.enter_context(tc.psum_pool(name="gbpsum", bufs=1))
         ypool = []
 
         ident = keep.tile([P, P], F32, name="ident")
@@ -73,8 +70,6 @@ def tile_coattention_pb_kernel(
         k1 = keep.tile([P, 1], F32, name="k1")
         k2 = keep.tile([P, 1], F32, name="k2")
         mv = keep.tile([P, NCT, 2], F32, name="mv")
-        g_ps = gbpsum.tile([P, D], BF16, name="g_ps")
-        b_ps = gbpsum.tile([P, D], BF16, name="b_ps")
 
         def mm(r, c):
             y = ypool[-1].tile([P, CHUNK], F32, name="y")
@@ -110,110 +105,116 @@ def tile_coattention_pb_kernel(
                 )
 
         nc.vector.memset(prm_bf[:], 0.0)
-        nc.sync.dma_start(out=prm_bf[0:NCT, :], in_=bn_v_g.rearrange("(c p) -> c p", p=P))
-        nc.sync.dma_start(out=prm_bf[NCT : 2 * NCT, :], in_=bn_v_b.rearrange("(c p) -> c p", p=P))
-        nc.sync.dma_start(out=prm_bf[2 * NCT : 3 * NCT, :], in_=ln_g.rearrange("(c p) -> c p", p=P))
-        nc.sync.dma_start(out=prm_bf[3 * NCT : 4 * NCT, :], in_=ln_b.rearrange("(c p) -> c p", p=P))
-        nc.sync.dma_start(out=a_bf[:], in_=prelu_v.partition_broadcast(P))
         with tc.tile_pool(name="wstage", bufs=1) as wstage, tc.tile_pool(name="cstage", bufs=2) as cstage, tc.psum_pool(
-            name="tpsum", bufs=2
-        ) as tpsum, tc.psum_pool(name="ypre", bufs=4) as ypre:
+            name="tpsum", bufs=3
+        ) as tpsum, tc.psum_pool(name="ypre", bufs=5) as ypre:
             ypool.append(ypre)
             w_raw = {}
             c_raw = {}
+            w_grp = {}
+            c_grp = {}
 
-            def load_w(h):
+            def load_w(h, pieces):
                 w_raw[h] = wstage.tile([P, HC, D], BF16, name="w_raw", bufs=2)
-                for q in range(2):
+                n = HC // pieces
+                for q in range(pieces):
                     nc.sync.dma_start(
-                        out=w_raw[h][:, 2 * q : 2 * q + 2, :],
-                        in_=W_v[(h * HC + 2 * q) * P : (h * HC + 2 * q + 2) * P, :].rearrange("(c p) k -> p c k", p=P),
+                        out=w_raw[h][:, n * q : n * (q + 1), :],
+                        in_=W_v[(h * HC + n * q) * P : (h * HC + n * (q + 1)) * P, :].rearrange("(c p) k -> p c k", p=P),
                     )
 
-            def load_ctx(r):
+            def load_ctx(r, pieces):
                 c_raw[r] = cstage.tile([P, B, D], BF16, name="c_raw", bufs=NCH)
-                nc.sync.dma_start(
-                    out=c_raw[r][:], in_=ctx_v[:, r * P : (r + 1) * P, :].rearrange("b l d -> l b d")
-                )
+                n = B // pieces
+                for q in range(pieces):
+                    nc.sync.dma_start(
+                        out=c_raw[r][:, n * q : n * (q + 1), :],
+                        in_=ctx_v[n * q : n * (q + 1), r * P : (r + 1) * P, :].rearrange("b l d -> l b d"),
+                    )
 
-            def turn(rows, grouped, on_vector):
-                words = rows.bitcast(F32)
+            def src_rows(kind, j):
+                return w_raw[j // HC][:, j % HC, :] if kind == "W" else c_raw[j // B][:, j % B, :]
+
+            def grp_of(kind, j):
+                if kind == "W":
+                    if j % HC == 0:
+                        w_grp[j // HC] = wstage.tile([P, NPASS, HW, 4], BF16, name="w_grp", align_bytes=64)
+                    return w_grp[j // HC]
+                if j % B == 0:
+                    c_grp[j // B] = cstage.tile([P, NPASS, CHUNK, 4], BF16, name="c_grp", align_bytes=64)
+                return c_grp[j // B]
+
+            def turn(kind, j, on_vector):
+                words = src_rows(kind, j).bitcast(F32)
                 tp = tpsum.tile([P, NPASS, 2, P], F32, name="tp")
                 for g in range(NPASS):
                     for u in range(2):
                         nc.tensor.transpose(tp[:, g, u, :], words[:, 256 * g + u : 256 * (g + 1) : 2], ident[:])
+                grouped = grp_of(kind, j)[:, :, (j % 4) * P : (j % 4 + 1) * P, :]
                 if on_vector:
                     nc.vector.tensor_copy(out=grouped.bitcast(F32), in_=tp[:].rearrange("p g u r -> p g r u"))
                 else:
                     nc.scalar.copy(out=grouped.bitcast(F32), in_=tp[:].rearrange("p g u r -> p g r u"))
 
-            def prep_w(h):
-                w_grp = wstage.tile([P, NPASS, HW, 4], BF16, name="w_grp", align_bytes=64)
-                for cc in range(HC):
-                    turn(w_raw[h][:, cc, :], w_grp[:, :, cc * P : (cc + 1) * P, :], h == 0 and cc % 2 == 0)
-                cols = slice(h * HW, (h + 1) * HW)
+            def quant(kind, j):
+                codes, scales = (w_codes, w_scales) if kind == "W" else (c_codes, c_scales)
+                grp = w_grp[j // 4] if kind == "W" else c_grp[j // 4]
                 for g in range(NPASS):
                     nc.vector.quantize_mx(
-                        out=w_codes[:, g, cols].bitcast(FP8X4),
-                        scales=w_scales[:, g, cols],
-                        in_=w_grp[:, g, :, :].rearrange("p c t -> p (c t)"),
-                    )
-
-            c_grp = {}
-
-            def turn_ctx(r):
-                c_grp[r] = cstage.tile([P, NPASS, CHUNK, 4], BF16, name="c_grp", align_bytes=64)
-                for b in range(B):
-                    turn(c_raw[r][:, b, :], c_grp[r][:, :, b * P : (b + 1) * P, :], False)
-
-            def quant_ctx(r):
-                cols = slice(r * CHUNK, (r + 1) * CHUNK)
-                for g in range(NPASS):
-                    nc.vector.quantize_mx(
-                        out=c_codes[:, g, cols].bitcast(FP8X4),
-                        scales=c_scales[:, g, cols],
-                        in_=c_grp[r][:, g, :, :].rearrange("p c t -> p (c t)"),
+                        out=codes[:, g, j * P : (j + 2) * P].bitcast(FP8X4),
+                        scales=scales[:, g, j * P : (j + 2) * P],
+                        in_=grp[:, g, (j % 4) * P : (j % 4 + 2) * P, :].rearrange("p c t -> p (c t)"),
                     )
 
             def aggr(c):
                 nc.vector.bn_aggr(out=mv[:, c, :], in_=bnst[:, c, :, :].rearrange("p r s -> p (r s)"))
 
-            def mm_stats(r):
-                for c in range(NCT):
-                    y = mm(r, c)
-                    nc.vector.bn_stats(out=bnst[:, c, r, :], in_=y[:])
-                    if c < HC:
-                        nc.scalar.copy(out=ysave[:, c, r * CHUNK : (r + 1) * CHUNK], in_=y[:])
-                    if c == HC - 1 and r + 1 < NCH:
-                        quant_ctx(r + 1)
-                    if r == NCH - 1 and c > 0:
-                        aggr(c - 1)
+            def mm_stat(r, c):
+                y = mm(r, c)
+                nc.vector.bn_stats(out=bnst[:, c, r, :], in_=y[:])
+                if c < HC:
+                    nc.scalar.copy(out=ysave[:, c, r * CHUNK : (r + 1) * CHUNK], in_=y[:])
+                if r == NCH - 1 and c > 0:
+                    aggr(c - 1)
 
-            load_w(0)
-            load_ctx(0)
-            nc.vector.tensor_copy(out=ident_bf[:], in_=ident[:])
-            nc.vector.tensor_copy(out=prm_f[:], in_=prm_bf[:])
-            prmT = tpsum.tile([P, NPASS, 2, P], F32, name="tp")
-            nc.tensor.transpose(prmT[:, 0, 0, :], prm_f[:], ident[:])
-            nc.vector.tensor_copy(out=lnT_bf[:], in_=prmT[:, 0, 0, 2 * NCT : 4 * NCT])
-            nc.vector.tensor_copy(out=gbT[:], in_=prmT[:, 0, 0, 0 : 2 * NCT])
-            for c in range(NCT):
-                nc.tensor.transpose(g_ps[:, c * P : (c + 1) * P], lnT_bf[:, c : c + 1].to_broadcast([P, P]), ident_bf[:])
-                nc.tensor.transpose(
-                    b_ps[:, c * P : (c + 1) * P], lnT_bf[:, NCT + c : NCT + c + 1].to_broadcast([P, P]), ident_bf[:]
-                )
-            nc.scalar.copy(out=g_sb[:], in_=g_ps[:])
-            load_w(1)
+            def unit(kind, j, mms):
+                turn(kind, j, False)
+                turn(kind, j + 1, False)
+                mm_stat(mms[0][0], mms[0][1])
+                quant(kind, j)
+                for rc in mms[1:]:
+                    mm_stat(rc[0], rc[1])
+
+            load_w(0, 4)
+            load_ctx(0, 4)
+            nc.sync.dma_start(out=prm_bf[0:NCT, :], in_=bn_v_g.rearrange("(c p) -> c p", p=P))
+            nc.sync.dma_start(out=prm_bf[NCT : 2 * NCT, :], in_=bn_v_b.rearrange("(c p) -> c p", p=P))
+            nc.sync.dma_start(out=prm_bf[2 * NCT : 3 * NCT, :], in_=ln_g.rearrange("(c p) -> c p", p=P))
+            nc.sync.dma_start(out=prm_bf[3 * NCT : 4 * NCT, :], in_=ln_b.rearrange("(c p) -> c p", p=P))
+            nc.sync.dma_start(out=a_bf[:], in_=prelu_v.partition_broadcast(P))
+            load_w(1, 2)
             for r in range(1, NCH):
-                load_ctx(r)
-            prep_w(0)
+                load_ctx(r, 1)
             load_xr(0, 0)
             load_xr(0, 1)
             load_xr(1, 0)
             load_xr(1, 1)
-            turn_ctx(0)
-            quant_ctx(0)
-            prep_w(1)
+            nc.sync.dma_start(out=g_sb[:], in_=ln_g.partition_broadcast(P))
+
+            turn("W", 0, True)
+            turn("W", 1, False)
+            turn("W", 2, True)
+            turn("W", 3, False)
+            quant("W", 0)
+            turn("X", 0, False)
+            turn("X", 1, True)
+            quant("W", 2)
+            turn("X", 2, False)
+            turn("X", 3, False)
+            quant("X", 0)
+            quant("X", 2)
+            nc.vector.tensor_copy(out=ident_bf[:], in_=ident[:])
+            nc.vector.tensor_copy(out=prm_f[:], in_=prm_bf[:])
             nc.vector.tensor_copy(out=a_f[:], in_=a_bf[:])
             nc.vector.tensor_scalar(out=sig[:], in0=a_f[:], scalar1=1.0, scalar2=-2.0, op0=ALU.is_gt, op1=ALU.mult)
             nc.vector.tensor_scalar(out=sig[:], in0=sig[:], scalar1=1.0, scalar2=None, op0=ALU.add)
@@ -221,14 +222,34 @@ def tile_coattention_pb_kernel(
             nc.vector.tensor_tensor(out=k1[:], in0=k1[:], in1=sig[:], op=ALU.mult)
             nc.vector.tensor_scalar(out=k2[:], in0=a_f[:], scalar1=-1.0, scalar2=1.0, op0=ALU.mult, op1=ALU.add)
             nc.vector.tensor_scalar(out=sI_bf[:], in0=ident[:], scalar1=sig[:, 0:1], scalar2=None, op0=ALU.mult)
-            for r in range(NCH):
-                if r + 1 < NCH:
-                    turn_ctx(r + 1)
-                mm_stats(r)
+            unit("W", 4, [(0, 0), (0, 1)])
+            unit("W", 6, [(0, 2), (0, 3)])
+            prmT = tpsum.tile([P, NPASS, 2, P], F32, name="tp")
+            nc.tensor.transpose(prmT[:, 0, 0, :], prm_f[:], ident[:])
+            nc.vector.tensor_copy(out=lnT_bf[:], in_=prmT[:, 0, 0, 2 * NCT : 4 * NCT])
+            nc.vector.tensor_copy(out=gbT[:], in_=prmT[:, 0, 0, 0 : 2 * NCT])
+            unit("X", 4, [(0, 4), (0, 5)])
+            unit("X", 6, [(0, 6), (0, 7)])
+            for r in range(1, NCH - 1):
+                unit("X", 4 * r + 4, [(r, c) for c in range(HC)])
+                unit("X", 4 * r + 6, [(r, c) for c in range(HC, NCT)])
+            for c in range(NCT):
+                mm_stat(NCH - 1, c)
             aggr(NCT - 1)
             for rh in ON_GPSIMD:
                 add_xr(rh[0], rh[1])
 
+        gbpsum = ctx.enter_context(tc.psum_pool(name="gbpsum", bufs=1))
+        g_ps = gbpsum.tile([P, D], BF16, name="g_ps")
+        b_ps = gbpsum.tile([P, D], BF16, name="b_ps")
+        for c in range(NCT):
+            nc.tensor.transpose(g_ps[:, c * P : (c + 1) * P], lnT_bf[:, c : c + 1].to_broadcast([P, P]), ident_bf[:])
+            nc.tensor.transpose(
+                b_ps[:, c * P : (c + 1) * P], lnT_bf[:, NCT + c : NCT + c + 1].to_broadcast([P, P]), ident_bf[:]
+            )
+
+        if MANUAL:
+            ctx.enter_context(tc.manual_schedule())
         bstd = keep.tile([P, NCT], F32, name="bstd")
         nc.scalar.activation(out=bstd[:], in_=mv[:, :, 1], func=ACT.Sqrt, bias=EPS_BN, scale=1.0)
         HALVES = (0, 1)

@@ -25,7 +25,6 @@ HW = HC * P
 NCH = L // P
 CHUNK = B * P
 NPASS = D // 512
-MANUAL = True
 ON_GPSIMD = ((0, 0), (0, 1))
 NGS = (3, 3, 3, 3)
 KV = 0
@@ -63,7 +62,6 @@ def tile_coattention_pb_kernel(
         a_bf = keep.tile([P, 1], BF16, name="a_bf")
         prm_bf = keep.tile([P, P], BF16, name="prm_bf")
         prm_f = keep.tile([P, P], F32, name="prm_f")
-        gbT = keep.tile([P, 2 * NCT], F32, name="gbT")
         sums = keep.tile([P, NCH, B, 2], F32, name="sums")
         a_f = keep.tile([P, 1], F32, name="a_f")
         sig = keep.tile([P, 1], F32, name="sig")
@@ -104,67 +102,61 @@ def tile_coattention_pb_kernel(
                     op=ALU.add,
                 )
 
+        HALVES = (0, 1)
+        gk = [keep.tile([P, NCT], F32, name="gk%d" % j) for j in (0, 1)]
+        bk = [keep.tile([P, NCT], F32, name="bk%d" % j) for j in (0, 1)]
+        bstd = [keep.tile([P, HC], F32, name="bstd%d" % h) for h in HALVES]
+        brstd = [keep.tile([P, HC], F32, name="brstd%d" % h) for h in HALVES]
+        psc = [[keep.tile([P, HC], F32, name="psc%d_%d" % (j, h)) for h in HALVES] for j in (0, 1)]
+        pmn = [[keep.tile([P, HC], F32, name="pmn%d_%d" % (j, h)) for h in HALVES] for j in (0, 1)]
+        pbi = [[keep.tile([P, HC], F32, name="pbi%d_%d" % (j, h)) for h in HALVES] for j in (0, 1)]
+        s12 = {}
+        ysrc = {}
+
+        def chain(h):
+            cs = slice(h * HC, (h + 1) * HC)
+            nc.scalar.activation(out=bstd[h][:], in_=mv[:, cs, 1], func=ACT.Sqrt, bias=EPS_BN, scale=1.0)
+            nc.vector.reciprocal(out=brstd[h][:], in_=bstd[h][:])
+            for j in (1, 0):
+                nc.vector.tensor_tensor(out=psc[j][h][:], in0=gk[j][:, cs], in1=brstd[h][:], op=ALU.mult)
+            for j in (1, 0):
+                nc.vector.tensor_tensor(out=pmn[j][h][:], in0=mv[:, cs, 0], in1=psc[j][h][:], op=ALU.mult)
+            for j in (1, 0):
+                nc.vector.tensor_tensor(out=pbi[j][h][:], in0=bk[j][:, cs], in1=pmn[j][h][:], op=ALU.subtract)
+
+        def src_of(r, h, cc):
+            return ysave[:, cc, r * CHUNK : (r + 1) * CHUNK] if h == 0 else ysrc[r, cc][:]
+
+        def new_block(r, h):
+            s12[r, h] = work.tile([P, 2, HC, CHUNK], F32, name="s12")
+
+        def s1(r, h, cc, eng):
+            if eng == "S":
+                nc.scalar.activation(
+                    out=s12[r, h][:, 0, cc, :], in_=src_of(r, h, cc), func=ACT.Identity,
+                    scale=psc[0][h][:, cc : cc + 1], bias=pbi[0][h][:, cc : cc + 1],
+                )
+            else:
+                (nc.vector if eng == "V" else nc.gpsimd).tensor_scalar(
+                    out=s12[r, h][:, 0, cc, :], in0=src_of(r, h, cc),
+                    scalar1=psc[0][h][:, cc : cc + 1], scalar2=pbi[0][h][:, cc : cc + 1], op0=ALU.mult, op1=ALU.add,
+                )
+
+        def s2(r, h, cc):
+            nc.scalar.activation(
+                out=s12[r, h][:, 1, cc, :], in_=src_of(r, h, cc), func=ACT.Relu,
+                scale=psc[1][h][:, cc : cc + 1], bias=pbi[1][h][:, cc : cc + 1],
+            )
+
+        def act0(r):
+            new_block(r, 0)
+            for cc in range(HC):
+                s1(r, 0, cc, "G")
+                s2(r, 0, cc)
+
         nc.vector.memset(prm_bf[:], 0.0)
-        with tc.tile_pool(name="wstage", bufs=1) as wstage, tc.tile_pool(name="cstage", bufs=2) as cstage, tc.psum_pool(
-            name="tpsum", bufs=3
-        ) as tpsum, tc.psum_pool(name="ypre", bufs=5) as ypre:
+        with tc.psum_pool(name="tpsum", bufs=3) as tpsum, tc.psum_pool(name="ypre", bufs=5) as ypre:
             ypool.append(ypre)
-            w_raw = {}
-            c_raw = {}
-            w_grp = {}
-            c_grp = {}
-
-            def load_w(h, pieces):
-                w_raw[h] = wstage.tile([P, HC, D], BF16, name="w_raw", bufs=2)
-                n = HC // pieces
-                for q in range(pieces):
-                    nc.sync.dma_start(
-                        out=w_raw[h][:, n * q : n * (q + 1), :],
-                        in_=W_v[(h * HC + n * q) * P : (h * HC + n * (q + 1)) * P, :].rearrange("(c p) k -> p c k", p=P),
-                    )
-
-            def load_ctx(r, pieces):
-                c_raw[r] = cstage.tile([P, B, D], BF16, name="c_raw", bufs=NCH)
-                n = B // pieces
-                for q in range(pieces):
-                    nc.sync.dma_start(
-                        out=c_raw[r][:, n * q : n * (q + 1), :],
-                        in_=ctx_v[n * q : n * (q + 1), r * P : (r + 1) * P, :].rearrange("b l d -> l b d"),
-                    )
-
-            def src_rows(kind, j):
-                return w_raw[j // HC][:, j % HC, :] if kind == "W" else c_raw[j // B][:, j % B, :]
-
-            def grp_of(kind, j):
-                if kind == "W":
-                    if j % HC == 0:
-                        w_grp[j // HC] = wstage.tile([P, NPASS, HW, 4], BF16, name="w_grp", align_bytes=64)
-                    return w_grp[j // HC]
-                if j % B == 0:
-                    c_grp[j // B] = cstage.tile([P, NPASS, CHUNK, 4], BF16, name="c_grp", align_bytes=64)
-                return c_grp[j // B]
-
-            def turn(kind, j, on_vector):
-                words = src_rows(kind, j).bitcast(F32)
-                tp = tpsum.tile([P, NPASS, 2, P], F32, name="tp")
-                for g in range(NPASS):
-                    for u in range(2):
-                        nc.tensor.transpose(tp[:, g, u, :], words[:, 256 * g + u : 256 * (g + 1) : 2], ident[:])
-                grouped = grp_of(kind, j)[:, :, (j % 4) * P : (j % 4 + 1) * P, :]
-                if on_vector:
-                    nc.vector.tensor_copy(out=grouped.bitcast(F32), in_=tp[:].rearrange("p g u r -> p g r u"))
-                else:
-                    nc.scalar.copy(out=grouped.bitcast(F32), in_=tp[:].rearrange("p g u r -> p g r u"))
-
-            def quant(kind, j):
-                codes, scales = (w_codes, w_scales) if kind == "W" else (c_codes, c_scales)
-                grp = w_grp[j // 4] if kind == "W" else c_grp[j // 4]
-                for g in range(NPASS):
-                    nc.vector.quantize_mx(
-                        out=codes[:, g, j * P : (j + 2) * P].bitcast(FP8X4),
-                        scales=scales[:, g, j * P : (j + 2) * P],
-                        in_=grp[:, g, (j % 4) * P : (j % 4 + 2) * P, :].rearrange("p c t -> p (c t)"),
-                    )
 
             def aggr(c):
                 nc.vector.bn_aggr(out=mv[:, c, :], in_=bnst[:, c, :, :].rearrange("p r s -> p (r s)"))
@@ -174,68 +166,140 @@ def tile_coattention_pb_kernel(
                 nc.vector.bn_stats(out=bnst[:, c, r, :], in_=y[:])
                 if c < HC:
                     nc.scalar.copy(out=ysave[:, c, r * CHUNK : (r + 1) * CHUNK], in_=y[:])
-                if r == NCH - 1 and c > 0:
-                    aggr(c - 1)
+                if r == NCH - 1:
+                    aggr(c)
 
-            def unit(kind, j, mms):
-                turn(kind, j, False)
-                turn(kind, j + 1, False)
-                mm_stat(mms[0][0], mms[0][1])
-                quant(kind, j)
-                for rc in mms[1:]:
-                    mm_stat(rc[0], rc[1])
+            with tc.tile_pool(name="wstage", bufs=1) as wstage, tc.tile_pool(name="cstage", bufs=2) as cstage:
+                w_raw = {}
+                c_raw = {}
+                w_grp = {}
+                c_grp = {}
 
-            load_w(0, 4)
-            load_ctx(0, 4)
-            nc.sync.dma_start(out=prm_bf[0:NCT, :], in_=bn_v_g.rearrange("(c p) -> c p", p=P))
-            nc.sync.dma_start(out=prm_bf[NCT : 2 * NCT, :], in_=bn_v_b.rearrange("(c p) -> c p", p=P))
-            nc.sync.dma_start(out=prm_bf[2 * NCT : 3 * NCT, :], in_=ln_g.rearrange("(c p) -> c p", p=P))
-            nc.sync.dma_start(out=prm_bf[3 * NCT : 4 * NCT, :], in_=ln_b.rearrange("(c p) -> c p", p=P))
-            nc.sync.dma_start(out=a_bf[:], in_=prelu_v.partition_broadcast(P))
-            load_w(1, 2)
-            for r in range(1, NCH):
-                load_ctx(r, 1)
-            load_xr(0, 0)
-            load_xr(0, 1)
-            load_xr(1, 0)
-            load_xr(1, 1)
-            nc.sync.dma_start(out=g_sb[:], in_=ln_g.partition_broadcast(P))
+                def load_w(h, pieces):
+                    w_raw[h] = wstage.tile([P, HC, D], BF16, name="w_raw", bufs=2)
+                    n = HC // pieces
+                    for q in range(pieces):
+                        nc.sync.dma_start(
+                            out=w_raw[h][:, n * q : n * (q + 1), :],
+                            in_=W_v[(h * HC + n * q) * P : (h * HC + n * (q + 1)) * P, :].rearrange(
+                                "(c p) k -> p c k", p=P
+                            ),
+                        )
 
-            turn("W", 0, True)
-            turn("W", 1, False)
-            turn("W", 2, True)
-            turn("W", 3, False)
-            quant("W", 0)
-            turn("X", 0, False)
-            turn("X", 1, True)
-            quant("W", 2)
-            turn("X", 2, False)
-            turn("X", 3, False)
-            quant("X", 0)
-            quant("X", 2)
-            nc.vector.tensor_copy(out=ident_bf[:], in_=ident[:])
-            nc.vector.tensor_copy(out=prm_f[:], in_=prm_bf[:])
-            nc.vector.tensor_copy(out=a_f[:], in_=a_bf[:])
-            nc.vector.tensor_scalar(out=sig[:], in0=a_f[:], scalar1=1.0, scalar2=-2.0, op0=ALU.is_gt, op1=ALU.mult)
-            nc.vector.tensor_scalar(out=sig[:], in0=sig[:], scalar1=1.0, scalar2=None, op0=ALU.add)
-            nc.vector.tensor_scalar(out=k1[:], in0=a_f[:], scalar1=1.0, scalar2=None, op0=ALU.min)
-            nc.vector.tensor_tensor(out=k1[:], in0=k1[:], in1=sig[:], op=ALU.mult)
-            nc.vector.tensor_scalar(out=k2[:], in0=a_f[:], scalar1=-1.0, scalar2=1.0, op0=ALU.mult, op1=ALU.add)
-            nc.vector.tensor_scalar(out=sI_bf[:], in0=ident[:], scalar1=sig[:, 0:1], scalar2=None, op0=ALU.mult)
-            unit("W", 4, [(0, 0), (0, 1)])
-            unit("W", 6, [(0, 2), (0, 3)])
-            prmT = tpsum.tile([P, NPASS, 2, P], F32, name="tp")
-            nc.tensor.transpose(prmT[:, 0, 0, :], prm_f[:], ident[:])
-            nc.vector.tensor_copy(out=lnT_bf[:], in_=prmT[:, 0, 0, 2 * NCT : 4 * NCT])
-            nc.vector.tensor_copy(out=gbT[:], in_=prmT[:, 0, 0, 0 : 2 * NCT])
-            unit("X", 4, [(0, 4), (0, 5)])
-            unit("X", 6, [(0, 6), (0, 7)])
-            for r in range(1, NCH - 1):
-                unit("X", 4 * r + 4, [(r, c) for c in range(HC)])
-                unit("X", 4 * r + 6, [(r, c) for c in range(HC, NCT)])
-            for c in range(NCT):
+                def load_ctx(r, pieces):
+                    c_raw[r] = cstage.tile([P, B, D], BF16, name="c_raw", bufs=NCH)
+                    n = B // pieces
+                    for q in range(pieces):
+                        nc.sync.dma_start(
+                            out=c_raw[r][:, n * q : n * (q + 1), :],
+                            in_=ctx_v[n * q : n * (q + 1), r * P : (r + 1) * P, :].rearrange("b l d -> l b d"),
+                        )
+
+                def grp_of(kind, j):
+                    if kind == "W":
+                        if j % HC == 0:
+                            w_grp[j // HC] = wstage.tile([P, NPASS, HW, 4], BF16, name="w_grp", align_bytes=64)
+                        return w_grp[j // HC]
+                    if j % B == 0:
+                        c_grp[j // B] = cstage.tile([P, NPASS, CHUNK, 4], BF16, name="c_grp", align_bytes=64)
+                    return c_grp[j // B]
+
+                def turn(kind, j, on_vector):
+                    rows = w_raw[j // HC][:, j % HC, :] if kind == "W" else c_raw[j // B][:, j % B, :]
+                    words = rows.bitcast(F32)
+                    tp = tpsum.tile([P, NPASS, 2, P], F32, name="tp")
+                    for g in range(NPASS):
+                        for u in range(2):
+                            nc.tensor.transpose(tp[:, g, u, :], words[:, 256 * g + u : 256 * (g + 1) : 2], ident[:])
+                    grouped = grp_of(kind, j)[:, :, (j % 4) * P : (j % 4 + 1) * P, :]
+                    if on_vector:
+                        nc.vector.tensor_copy(out=grouped.bitcast(F32), in_=tp[:].rearrange("p g u r -> p g r u"))
+                    else:
+                        nc.scalar.copy(out=grouped.bitcast(F32), in_=tp[:].rearrange("p g u r -> p g r u"))
+
+                def quant(kind, j, n):
+                    codes, scales = (w_codes, w_scales) if kind == "W" else (c_codes, c_scales)
+                    grp = w_grp[j // 4] if kind == "W" else c_grp[j // 4]
+                    for g in range(NPASS):
+                        nc.vector.quantize_mx(
+                            out=codes[:, g, j * P : (j + n) * P].bitcast(FP8X4),
+                            scales=scales[:, g, j * P : (j + n) * P],
+                            in_=grp[:, g, (j % 4) * P : (j % 4 + n) * P, :].rearrange("p c t -> p (c t)"),
+                        )
+
+                load_ctx(0, 4)
+                load_w(0, 4)
+                load_w(1, 4)
+                nc.sync.dma_start(out=prm_bf[0:NCT, :], in_=bn_v_g.rearrange("(c p) -> c p", p=P))
+                nc.sync.dma_start(out=prm_bf[NCT : 2 * NCT, :], in_=bn_v_b.rearrange("(c p) -> c p", p=P))
+                nc.sync.dma_start(out=prm_bf[2 * NCT : 3 * NCT, :], in_=ln_g.rearrange("(c p) -> c p", p=P))
+                nc.sync.dma_start(out=prm_bf[3 * NCT : 4 * NCT, :], in_=ln_b.rearrange("(c p) -> c p", p=P))
+                nc.sync.dma_start(out=a_bf[:], in_=prelu_v.partition_broadcast(P))
+                for r in range(1, NCH):
+                    load_ctx(r, 2)
+                load_xr(0, 0)
+                load_xr(0, 1)
+                load_xr(1, 0)
+                load_xr(1, 1)
+                nc.sync.dma_start(out=g_sb[:], in_=ln_g.partition_broadcast(P))
+
+                def unit(kind, j, mms):
+                    turn(kind, j, False)
+                    turn(kind, j + 1, False)
+                    mm_stat(mms[0][0], mms[0][1])
+                    quant(kind, j, 2)
+                    for rc in mms[1:]:
+                        mm_stat(rc[0], rc[1])
+
+                for b in range(B):
+                    turn("X", b, b % 2 == 1)
+                    if b % 2 == 1:
+                        quant("X", b - 1, 2)
+                for c in range(2):
+                    turn("W", c, False)
+                    quant("W", c, 1)
+                    mm_stat(0, c)
+                for c in range(2, NCT, 2):
+                    turn("W", c, False)
+                    turn("W", c + 1, False)
+                    quant("W", c, 2)
+                    mm_stat(0, c)
+                    mm_stat(0, c + 1)
+                    if c >= HC:
+                        turn("X", c, False)
+                        turn("X", c + 1, False)
+                        quant("X", c, 2)
+                nc.vector.tensor_copy(out=ident_bf[:], in_=ident[:])
+                nc.vector.tensor_copy(out=prm_f[:], in_=prm_bf[:])
+                nc.vector.tensor_copy(out=a_f[:], in_=a_bf[:])
+                nc.vector.tensor_scalar(out=sig[:], in0=a_f[:], scalar1=1.0, scalar2=-2.0, op0=ALU.is_gt, op1=ALU.mult)
+                nc.vector.tensor_scalar(out=sig[:], in0=sig[:], scalar1=1.0, scalar2=None, op0=ALU.add)
+                nc.vector.tensor_scalar(out=k1[:], in0=a_f[:], scalar1=1.0, scalar2=None, op0=ALU.min)
+                nc.vector.tensor_tensor(out=k1[:], in0=k1[:], in1=sig[:], op=ALU.mult)
+                nc.vector.tensor_scalar(out=k2[:], in0=a_f[:], scalar1=-1.0, scalar2=1.0, op0=ALU.mult, op1=ALU.add)
+                nc.vector.tensor_scalar(out=sI_bf[:], in0=ident[:], scalar1=sig[:, 0:1], scalar2=None, op0=ALU.mult)
+                prmT = tpsum.tile([P, NPASS, 2, P], F32, name="tp")
+                nc.tensor.transpose(prmT[:, 0, 0, :], prm_f[:], ident[:])
+                nc.vector.tensor_copy(out=lnT_bf[:], in_=prmT[:, 0, 0, 2 * NCT : 4 * NCT])
+                for j in (0, 1):
+                    kj = k1 if j == 0 else k2
+                    nc.vector.tensor_scalar(
+                        out=gk[j][:], in0=prmT[:, 0, 0, 0:NCT], scalar1=kj[:, 0:1], scalar2=None, op0=ALU.mult
+                    )
+                    nc.vector.tensor_scalar(
+                        out=bk[j][:], in0=prmT[:, 0, 0, NCT : 2 * NCT], scalar1=kj[:, 0:1], scalar2=None, op0=ALU.mult
+                    )
+                for r in range(1, NCH - 1):
+                    unit("X", B * r + B, [(r, c) for c in range(HC)])
+                    unit("X", B * r + B + 2, [(r, c) for c in range(HC, NCT)])
+            work = ctx.enter_context(tc.tile_pool(name="work", bufs=2))
+            for c in range(HC):
                 mm_stat(NCH - 1, c)
-            aggr(NCT - 1)
+            chain(0)
+            act0(0)
+            for c in range(HC, NCT):
+                mm_stat(NCH - 1, c)
+            chain(1)
             for rh in ON_GPSIMD:
                 add_xr(rh[0], rh[1])
 
@@ -248,36 +312,9 @@ def tile_coattention_pb_kernel(
                 b_ps[:, c * P : (c + 1) * P], lnT_bf[:, NCT + c : NCT + c + 1].to_broadcast([P, P]), ident_bf[:]
             )
 
-        if MANUAL:
-            ctx.enter_context(tc.manual_schedule())
-        bstd = keep.tile([P, NCT], F32, name="bstd")
-        nc.scalar.activation(out=bstd[:], in_=mv[:, :, 1], func=ACT.Sqrt, bias=EPS_BN, scale=1.0)
-        HALVES = (0, 1)
-        brstd = [keep.tile([P, HC], F32, name="brstd%d" % h) for h in HALVES]
-        st = [keep.tile([P, 2, HC], F32, name="st%d" % h) for h in HALVES]
-        ms = [keep.tile([P, HC], F32, name="ms%d" % h) for h in HALVES]
-        p1 = [keep.tile([P, 2, HC], F32, name="p1_%d" % h) for h in HALVES]
-        p2 = [keep.tile([P, 2, HC], F32, name="p2_%d" % h) for h in HALVES]
-        for h in HALVES:
-            nc.vector.reciprocal(out=brstd[h][:], in_=bstd[:, h * HC : (h + 1) * HC])
-        for h in HALVES:
-            nc.vector.tensor_tensor(out=st[h][:, 0, :], in0=gbT[:, h * HC : (h + 1) * HC], in1=brstd[h][:], op=ALU.mult)
-        for h in HALVES:
-            nc.vector.tensor_tensor(out=ms[h][:], in0=mv[:, h * HC : (h + 1) * HC, 0], in1=st[h][:, 0, :], op=ALU.mult)
-        for h in HALVES:
-            nc.vector.tensor_tensor(
-                out=st[h][:, 1, :], in0=gbT[:, NCT + h * HC : NCT + (h + 1) * HC], in1=ms[h][:], op=ALU.subtract
-            )
-        for h in HALVES:
-            nc.vector.tensor_scalar(out=p2[h][:], in0=st[h][:], scalar1=k2[:, 0:1], scalar2=None, op0=ALU.mult)
-        for h in HALVES:
-            nc.vector.tensor_scalar(out=p1[h][:], in0=st[h][:], scalar1=k1[:, 0:1], scalar2=None, op0=ALU.mult)
-
-        work = ctx.enter_context(tc.tile_pool(name="work", bufs=2))
+        ctx.enter_context(tc.manual_schedule())
         opsum = ctx.enter_context(tc.psum_pool(name="opsum", bufs=3))
         ypool.append(ctx.enter_context(tc.psum_pool(name="ypost", bufs=3)))
-        s12 = {}
-        ysrc = {}
         negmu = {}
         stdv = {}
         t1 = {}
@@ -286,36 +323,6 @@ def tile_coattention_pb_kernel(
         def mm_f(r, ccs):
             for cc in ccs:
                 ysrc[r, cc] = mm(r, HC + cc)
-
-        def src_of(r, h, cc):
-            return ysave[:, cc, r * CHUNK : (r + 1) * CHUNK] if h == 0 else ysrc[r, cc][:]
-
-        def new_block(r, h):
-            s12[r, h] = work.tile([P, 2, HC, CHUNK], F32, name="s12")
-
-        def s1(r, h, cc, eng):
-            if eng == "S":
-                nc.scalar.activation(
-                    out=s12[r, h][:, 0, cc, :], in_=src_of(r, h, cc), func=ACT.Identity,
-                    scale=p1[h][:, 0, cc : cc + 1], bias=p1[h][:, 1, cc : cc + 1],
-                )
-            else:
-                (nc.vector if eng == "V" else nc.gpsimd).tensor_scalar(
-                    out=s12[r, h][:, 0, cc, :], in0=src_of(r, h, cc),
-                    scalar1=p1[h][:, 0, cc : cc + 1], scalar2=p1[h][:, 1, cc : cc + 1], op0=ALU.mult, op1=ALU.add,
-                )
-
-        def s2(r, h, cc):
-            nc.scalar.activation(
-                out=s12[r, h][:, 1, cc, :], in_=src_of(r, h, cc), func=ACT.Relu,
-                scale=p2[h][:, 0, cc : cc + 1], bias=p2[h][:, 1, cc : cc + 1],
-            )
-
-        def act0(r):
-            new_block(r, 0)
-            for cc in range(HC):
-                s1(r, 0, cc, "G")
-                s2(r, 0, cc)
 
         def act1(r, ccs):
             for cc in ccs:
@@ -467,7 +474,7 @@ def tile_coattention_pb_kernel(
                 if has(i + 3):
                     load_xr(i + 3, 0)
                     load_xr(i + 3, 1)
-            if has(i + 2):
+            if has(i + 2) and i + 2 > 0:
                 act0(i + 2)
             if has(i):
                 casts(i, 0)

@@ -26,7 +26,7 @@ NCH = L // P
 CHUNK = B * P
 NPASS = D // 512
 ON_GPSIMD = ((0, 0), (0, 1))
-NGS = (3, 3, 3, 3)
+NGS = (3, 3, 3, 2)
 KV = 0
 
 
@@ -46,7 +46,7 @@ def tile_coattention_pb_kernel(
         zero = keep.tile([P, 1], F32, name="zero")
         nc.vector.memset(zero[:], 0.0)
         warm = keep.tile([P, 1], F32, name="warm")
-        nc.scalar.activation(out=warm[:], in_=one[:], func=ACT.Sqrt)
+        nc.scalar.activation(out=warm[:], in_=one[:], func=ACT.Abs_reciprocal_sqrt)
 
         w_codes = keep.tile([P, NPASS, D], U32, name="w_codes", align_bytes=64)
         w_scales = keep.tile([P, NPASS, D], U8, name="w_scales", align_bytes=64)
@@ -105,7 +105,6 @@ def tile_coattention_pb_kernel(
         HALVES = (0, 1)
         gk = [keep.tile([P, NCT], F32, name="gk%d" % j) for j in (0, 1)]
         bk = [keep.tile([P, NCT], F32, name="bk%d" % j) for j in (0, 1)]
-        bstd = [keep.tile([P, HC], F32, name="bstd%d" % h) for h in HALVES]
         brstd = [keep.tile([P, HC], F32, name="brstd%d" % h) for h in HALVES]
         psc = [[keep.tile([P, HC], F32, name="psc%d_%d" % (j, h)) for h in HALVES] for j in (0, 1)]
         pmn = [[keep.tile([P, HC], F32, name="pmn%d_%d" % (j, h)) for h in HALVES] for j in (0, 1)]
@@ -115,8 +114,7 @@ def tile_coattention_pb_kernel(
 
         def chain(h):
             cs = slice(h * HC, (h + 1) * HC)
-            nc.scalar.activation(out=bstd[h][:], in_=mv[:, cs, 1], func=ACT.Sqrt, bias=EPS_BN, scale=1.0)
-            nc.vector.reciprocal(out=brstd[h][:], in_=bstd[h][:])
+            nc.scalar.activation(out=brstd[h][:], in_=mv[:, cs, 1], func=ACT.Abs_reciprocal_sqrt, bias=EPS_BN, scale=1.0)
             for j in (1, 0):
                 nc.vector.tensor_tensor(out=psc[j][h][:], in0=gk[j][:, cs], in1=brstd[h][:], op=ALU.mult)
             for j in (1, 0):
@@ -374,8 +372,10 @@ def tile_coattention_pb_kernel(
                     out=junk[:], in_=o_t[r][b][:], func=ACT.Square,
                     bias=negmu[r][:, b : b + 1], scale=1.0, accum_out=ssq[:, b : b + 1],
                 )
-            stdv[r] = work.tile([P, B], F32, name="stdv")
-            nc.scalar.activation(out=stdv[r][:], in_=ssq[:], func=ACT.Sqrt, bias=EPS_LN, scale=1.0 / D)
+            stdv[r] = work.tile([P, B], F32, name="rstd")
+            nc.scalar.activation(
+                out=stdv[r][:], in_=ssq[:], func=ACT.Abs_reciprocal_sqrt, bias=EPS_LN, scale=1.0 / D
+            )
 
         def stt1_g(r):
             for b in range(B - NGS[r], B):
@@ -395,8 +395,7 @@ def tile_coattention_pb_kernel(
                 )
 
         def ln_open(r):
-            lnt[r] = [work.tile([P, B], F32, name=n) for n in ("rstd", "amax", "ram", "r448")]
-            nc.vector.reciprocal(out=lnt[r][0][:], in_=stdv[r][:])
+            lnt[r] = [stdv[r]] + [work.tile([P, B], F32, name=n) for n in ("amax", "ram", "r448")]
 
         def stt2(r, b):
             nc.vector.scalar_tensor_tensor(
@@ -413,23 +412,26 @@ def tile_coattention_pb_kernel(
         def rec(r, q):
             nc.vector.reciprocal(out=lnt[r][2][:, 2 * q : 2 * q + 2], in_=lnt[r][1][:, 2 * q : 2 * q + 2])
 
+        def cast(r, b, on_vector):
+            f8 = work.tile([P, D], FP8, name="f8", bufs=4)
+            if on_vector:
+                nc.vector.tensor_scalar(
+                    out=f8[:], in0=o_t[r][b][:], scalar1=lnt[r][3][:, b : b + 1], scalar2=None, op0=ALU.mult,
+                    saturate=False,
+                )
+            else:
+                nc.scalar.activation(
+                    out=f8[:], in_=o_t[r][b][:], func=ACT.Identity,
+                    scale=lnt[r][3][:, b : b + 1], bias=zero[:, 0:1], saturate=False,
+                )
+            nc.sync.dma_start(out=out_1[r * P : (r + 1) * P, b, :], in_=f8[:].bitcast(U8))
+
         def casts(r, q):
             nc.scalar.activation(
                 out=lnt[r][3][:, 2 * q : 2 * q + 2], in_=lnt[r][2][:, 2 * q : 2 * q + 2], func=ACT.Copy, scale=448.0
             )
             for b in (2 * q, 2 * q + 1):
-                f8 = work.tile([P, D], FP8, name="f8", bufs=4)
-                if r == NCH - 1 and b == B - 1:
-                    nc.vector.tensor_scalar(
-                        out=f8[:], in0=o_t[r][b][:], scalar1=lnt[r][3][:, b : b + 1], scalar2=None, op0=ALU.mult,
-                        saturate=False,
-                    )
-                else:
-                    nc.scalar.activation(
-                        out=f8[:], in_=o_t[r][b][:], func=ACT.Identity,
-                        scale=lnt[r][3][:, b : b + 1], bias=zero[:, 0:1], saturate=False,
-                    )
-                nc.sync.dma_start(out=out_1[r * P : (r + 1) * P, b, :], in_=f8[:].bitcast(U8))
+                cast(r, b, False)
 
         def ln_half(r, q):
             stt2(r, 2 * q)
@@ -484,7 +486,16 @@ def tile_coattention_pb_kernel(
             if has(i + 2):
                 mm_f(i + 2, (0, 1, 2))
                 tr(i + 2, 0, (0, 1, 2))
-            if has(i):
+            if has(i) and i < NCH - 1:
                 ln_half(i, 1)
-        rec(NCH - 1, 1)
-        casts(NCH - 1, 1)
+        r = NCH - 1
+        stt2(r, 2)
+        stt2(r, 3)
+        amx(r, 2)
+        nc.vector.reciprocal(out=lnt[r][2][:, 2:3], in_=lnt[r][1][:, 2:3])
+        amx(r, 3)
+        nc.scalar.activation(out=lnt[r][3][:, 2:3], in_=lnt[r][2][:, 2:3], func=ACT.Copy, scale=448.0)
+        cast(r, 2, False)
+        nc.vector.reciprocal(out=lnt[r][2][:, 3:4], in_=lnt[r][1][:, 3:4])
+        nc.vector.tensor_scalar(out=lnt[r][3][:, 3:4], in0=lnt[r][2][:, 3:4], scalar1=448.0, scalar2=None, op0=ALU.mult)
+        cast(r, 3, True)

@@ -27,7 +27,7 @@ CHUNK = B * P
 NPASS = D // 512
 ON_GPSIMD = ((0, 0), (0, 1))
 NGS = (3, 3, 3, 2)
-KV = 0
+HS = 6
 
 
 def tile_coattention_pb_kernel(
@@ -53,8 +53,8 @@ def tile_coattention_pb_kernel(
         c_codes = keep.tile([P, NPASS, NCH * CHUNK], U32, name="c_codes", align_bytes=64)
         c_scales = keep.tile([P, NPASS, NCH * CHUNK], U8, name="c_scales", align_bytes=64)
         bnst = keep.tile([P, NCT, NCH, 6], F32, name="bnst")
-        ysave = keep.tile([P, HC, NCH * CHUNK], F32, name="ysave")
-        o_t = [[keep.tile([P, D], F32, name="o_%d_%d" % (r, b)) for b in range(B)] for r in range(NCH)]
+        ysave = keep.tile([P, HS, NCH * CHUNK], F32, name="ysave")
+        o_t = [[keep.tile([P, D], F32, name="o_%d_%d" % (r, b)) for b in range(B)] for r in range(1)]
         g_sb = keep.tile([P, D], BF16, name="g_sb")
         ident_bf = keep.tile([P, P], BF16, name="ident_bf")
         sI_bf = keep.tile([P, P], BF16, name="sI_bf")
@@ -123,7 +123,8 @@ def tile_coattention_pb_kernel(
                 nc.vector.tensor_tensor(out=pbi[j][h][:], in0=bk[j][:, cs], in1=pmn[j][h][:], op=ALU.subtract)
 
         def src_of(r, h, cc):
-            return ysave[:, cc, r * CHUNK : (r + 1) * CHUNK] if h == 0 else ysrc[r, cc][:]
+            c = h * HC + cc
+            return ysave[:, c, r * CHUNK : (r + 1) * CHUNK] if c < HS else ysrc[r, cc][:]
 
         def new_block(r, h):
             s12[r, h] = work.tile([P, 2, HC, CHUNK], F32, name="s12")
@@ -162,7 +163,7 @@ def tile_coattention_pb_kernel(
             def mm_stat(r, c):
                 y = mm(r, c)
                 nc.vector.bn_stats(out=bnst[:, c, r, :], in_=y[:])
-                if c < HC:
+                if c < HS:
                     nc.scalar.copy(out=ysave[:, c, r * CHUNK : (r + 1) * CHUNK], in_=y[:])
                 if r == NCH - 1:
                     aggr(c)
@@ -291,6 +292,8 @@ def tile_coattention_pb_kernel(
                     unit("X", B * r + B, [(r, c) for c in range(HC)])
                     unit("X", B * r + B + 2, [(r, c) for c in range(HC, NCT)])
             work = ctx.enter_context(tc.tile_pool(name="work", bufs=2))
+            for r in range(1, NCH):
+                o_t.append([work.tile([P, D], F32, name="o_%d_%d" % (r, b), bufs=1) for b in range(B)])
             for c in range(HC):
                 mm_stat(NCH - 1, c)
             chain(0)
@@ -311,8 +314,8 @@ def tile_coattention_pb_kernel(
             )
 
         ctx.enter_context(tc.manual_schedule())
-        opsum = ctx.enter_context(tc.psum_pool(name="opsum", bufs=3))
-        ypool.append(ctx.enter_context(tc.psum_pool(name="ypost", bufs=3)))
+        opsum = ctx.enter_context(tc.psum_pool(name="opsum", bufs=4))
+        ypool.append(ctx.enter_context(tc.psum_pool(name="ypost", bufs=2)))
         negmu = {}
         stdv = {}
         t1 = {}
@@ -320,12 +323,18 @@ def tile_coattention_pb_kernel(
 
         def mm_f(r, ccs):
             for cc in ccs:
-                ysrc[r, cc] = mm(r, HC + cc)
+                if HC + cc >= HS:
+                    ysrc[r, cc] = mm(r, HC + cc)
 
         def act1(r, ccs):
             for cc in ccs:
                 s2(r, 1, cc)
-                s1(r, 1, cc, "V" if cc < KV else "S")
+                if HC + cc >= HS:
+                    s1(r, 1, cc, "S")
+
+        def act1_g(r):
+            for cc in range(HS - HC):
+                s1(r, 1, cc, "G")
 
         ots = {}
 
@@ -379,7 +388,7 @@ def tile_coattention_pb_kernel(
 
         def stt1_g(r):
             for b in range(B - NGS[r], B):
-                t1[r, b] = work.tile([P, D], F32, name="t1g", bufs=6)
+                t1[r, b] = work.tile([P, D], F32, name="t1g", bufs=3)
                 nc.gpsimd.tensor_scalar(
                     out=t1[r, b][:], in0=o_t[r][b][:], scalar1=negmu[r][:, b : b + 1], scalar2=1.0,
                     op0=ALU.add, op1=ALU.mult,
@@ -444,7 +453,6 @@ def tile_coattention_pb_kernel(
 
         for i in range(-2, NCH):
             if has(i + 1):
-                new_block(i + 1, 1)
                 act1(i + 1, (0,))
             if has(i):
                 stt1_v(i)
@@ -452,8 +460,6 @@ def tile_coattention_pb_kernel(
                 rec(i - 1, 1)
             if has(i + 1):
                 ev(i + 1, 0, (0,))
-                tr(i + 1, 0, (3,))
-                mm_f(i + 1, (3,))
                 act1(i + 1, (1, 2, 3))
                 ev(i + 1, 0, (1, 2))
             if has(i):
@@ -465,12 +471,11 @@ def tile_coattention_pb_kernel(
             if has(i):
                 ln_half(i, 0)
             if has(i + 1):
-                tr(i + 1, 1, (0, 1, 2))
+                tr(i + 1, 1, (0, 1, 2, 3))
                 ev(i + 1, 1, (0,))
             if has(i):
                 rec(i, 0)
             if has(i + 1):
-                tr(i + 1, 1, (3,))
                 ev(i + 1, 1, (1, 2, 3))
                 total(i + 1)
                 if has(i + 3):
@@ -478,14 +483,17 @@ def tile_coattention_pb_kernel(
                     load_xr(i + 3, 1)
             if has(i + 2) and i + 2 > 0:
                 act0(i + 2)
+            if has(i + 2):
+                new_block(i + 2, 1)
+                act1_g(i + 2)
             if has(i):
                 casts(i, 0)
             if has(i + 1):
                 stats(i + 1)
                 stt1_g(i + 1)
             if has(i + 2):
-                mm_f(i + 2, (0, 1, 2))
-                tr(i + 2, 0, (0, 1, 2))
+                mm_f(i + 2, (0, 1, 2, 3))
+                tr(i + 2, 0, (0, 1, 2, 3))
             if has(i) and i < NCH - 1:
                 ln_half(i, 1)
         r = NCH - 1

@@ -26,7 +26,8 @@ NCH = L // P
 CHUNK = B * P
 NPASS = D // 512
 ON_GPSIMD = ((0, 0), (0, 1))
-NGS = (3, 3, 3, 2)
+NGS = (2, 3, 3, 3)
+NSS = 1
 HS = 6
 
 
@@ -68,6 +69,14 @@ def tile_coattention_pb_kernel(
         k1 = keep.tile([P, 1], F32, name="k1")
         k2 = keep.tile([P, 1], F32, name="k2")
         mv = keep.tile([P, NCT, 2], F32, name="mv")
+        sy = keep.tile([P, NSS, NCH], F32, name="sy")
+        sq = keep.tile([P, NSS, NCH], F32, name="sq")
+        negm0 = keep.tile([P, NSS], F32, name="negm0")
+        toty = keep.tile([P, NSS], F32, name="toty")
+        totq = keep.tile([P, NSS], F32, name="totq")
+        dm = keep.tile([P, NSS], F32, name="dm")
+        dm2 = keep.tile([P, NSS], F32, name="dm2")
+        sjunk = keep.tile([P, CHUNK], BF16, name="sjunk")
 
         def mm(r, c):
             y = ypool[-1].tile([P, CHUNK], F32, name="y")
@@ -160,8 +169,41 @@ def tile_coattention_pb_kernel(
             def aggr(c):
                 nc.vector.bn_aggr(out=mv[:, c, :], in_=bnst[:, c, :, :].rearrange("p r s -> p (r s)"))
 
+            def square(r, c):
+                nc.scalar.activation(
+                    out=sjunk[:], in_=ysave[:, c, r * CHUNK : (r + 1) * CHUNK], func=ACT.Square,
+                    bias=negm0[:, c : c + 1], scale=1.0, accum_out=sq[:, c, r : r + 1],
+                )
+
+            def scalar_stats():
+                n_rows = NCH * CHUNK
+                nc.vector.tensor_reduce(out=toty[:], in_=sy[:], axis=AX.X, op=ALU.add)
+                nc.vector.tensor_reduce(out=totq[:], in_=sq[:], axis=AX.X, op=ALU.add)
+                nc.vector.tensor_scalar(
+                    out=mv[:, 0:NSS, 0], in0=toty[:], scalar1=1.0 / n_rows, scalar2=None, op0=ALU.mult
+                )
+                nc.vector.scalar_tensor_tensor(
+                    out=dm[:], in0=toty[:], scalar=1.0 / n_rows, in1=negm0[:], op0=ALU.mult, op1=ALU.add
+                )
+                nc.vector.tensor_tensor(out=dm2[:], in0=dm[:], in1=dm[:], op=ALU.mult)
+                nc.vector.scalar_tensor_tensor(
+                    out=mv[:, 0:NSS, 1], in0=totq[:], scalar=1.0 / n_rows, in1=dm2[:], op0=ALU.mult, op1=ALU.subtract
+                )
+
             def mm_stat(r, c):
                 y = mm(r, c)
+                if c < NSS:
+                    nc.scalar.activation(
+                        out=ysave[:, c, r * CHUNK : (r + 1) * CHUNK], in_=y[:], func=ACT.Copy,
+                        accum_out=sy[:, c, r : r + 1],
+                    )
+                    if r > 0:
+                        square(r, c)
+                    elif c == NSS - 1:
+                        nc.scalar.activation(out=negm0[:], in_=sy[:, :, 0], func=ACT.Copy, scale=-1.0 / CHUNK)
+                        for c0 in range(NSS):
+                            square(0, c0)
+                    return
                 nc.vector.bn_stats(out=bnst[:, c, r, :], in_=y[:])
                 if c < HS:
                     nc.scalar.copy(out=ysave[:, c, r * CHUNK : (r + 1) * CHUNK], in_=y[:])
@@ -268,25 +310,23 @@ def tile_coattention_pb_kernel(
                         turn("X", c, False)
                         turn("X", c + 1, False)
                         quant("X", c, 2)
-                nc.vector.tensor_copy(out=ident_bf[:], in_=ident[:])
-                nc.vector.tensor_copy(out=prm_f[:], in_=prm_bf[:])
-                nc.vector.tensor_copy(out=a_f[:], in_=a_bf[:])
-                nc.vector.tensor_scalar(out=sig[:], in0=a_f[:], scalar1=1.0, scalar2=-2.0, op0=ALU.is_gt, op1=ALU.mult)
-                nc.vector.tensor_scalar(out=sig[:], in0=sig[:], scalar1=1.0, scalar2=None, op0=ALU.add)
-                nc.vector.tensor_scalar(out=k1[:], in0=a_f[:], scalar1=1.0, scalar2=None, op0=ALU.min)
-                nc.vector.tensor_tensor(out=k1[:], in0=k1[:], in1=sig[:], op=ALU.mult)
-                nc.vector.tensor_scalar(out=k2[:], in0=a_f[:], scalar1=-1.0, scalar2=1.0, op0=ALU.mult, op1=ALU.add)
-                nc.vector.tensor_scalar(out=sI_bf[:], in0=ident[:], scalar1=sig[:, 0:1], scalar2=None, op0=ALU.mult)
+                nc.gpsimd.tensor_copy(out=ident_bf[:], in_=ident[:])
+                nc.gpsimd.tensor_copy(out=prm_f[:], in_=prm_bf[:])
+                nc.gpsimd.tensor_copy(out=a_f[:], in_=a_bf[:])
+                nc.gpsimd.tensor_scalar(out=sig[:], in0=a_f[:], scalar1=1.0, scalar2=-2.0, op0=ALU.is_gt, op1=ALU.mult)
+                nc.gpsimd.tensor_scalar(out=sig[:], in0=sig[:], scalar1=1.0, scalar2=None, op0=ALU.add)
+                nc.gpsimd.tensor_scalar(out=k1[:], in0=a_f[:], scalar1=1.0, scalar2=None, op0=ALU.min)
+                nc.gpsimd.tensor_tensor(out=k1[:], in0=k1[:], in1=sig[:], op=ALU.mult)
+                nc.gpsimd.tensor_scalar(out=k2[:], in0=a_f[:], scalar1=-1.0, scalar2=1.0, op0=ALU.mult, op1=ALU.add)
+                nc.gpsimd.tensor_scalar(out=sI_bf[:], in0=ident[:], scalar1=sig[:, 0:1], scalar2=None, op0=ALU.mult)
                 prmT = tpsum.tile([P, NPASS, 2, P], F32, name="tp")
                 nc.tensor.transpose(prmT[:, 0, 0, :], prm_f[:], ident[:])
-                nc.vector.tensor_copy(out=lnT_bf[:], in_=prmT[:, 0, 0, 2 * NCT : 4 * NCT])
+                nc.scalar.copy(out=lnT_bf[:], in_=prmT[:, 0, 0, 2 * NCT : 4 * NCT])
                 for j in (0, 1):
                     kj = k1 if j == 0 else k2
-                    nc.vector.tensor_scalar(
-                        out=gk[j][:], in0=prmT[:, 0, 0, 0:NCT], scalar1=kj[:, 0:1], scalar2=None, op0=ALU.mult
-                    )
-                    nc.vector.tensor_scalar(
-                        out=bk[j][:], in0=prmT[:, 0, 0, NCT : 2 * NCT], scalar1=kj[:, 0:1], scalar2=None, op0=ALU.mult
+                    nc.scalar.activation(out=gk[j][:], in_=prmT[:, 0, 0, 0:NCT], func=ACT.Copy, scale=kj[:, 0:1])
+                    nc.scalar.activation(
+                        out=bk[j][:], in_=prmT[:, 0, 0, NCT : 2 * NCT], func=ACT.Copy, scale=kj[:, 0:1]
                     )
                 for r in range(1, NCH - 1):
                     unit("X", B * r + B, [(r, c) for c in range(HC)])
@@ -296,6 +336,7 @@ def tile_coattention_pb_kernel(
                 o_t.append([work.tile([P, D], F32, name="o_%d_%d" % (r, b), bufs=1) for b in range(B)])
             for c in range(HC):
                 mm_stat(NCH - 1, c)
+            scalar_stats()
             chain(0)
             act0(0)
             for c in range(HC, NCT):

@@ -1,3 +1,4 @@
+import math
 from contextlib import ExitStack
 
 import concourse.mybir as mybir
@@ -459,9 +460,6 @@ def tile_coattention_pb_kernel(
                 out=lnt[r][1][:, b : b + 1], in_=o_t[r][b][:], axis=AX.X, op=ALU.max, apply_absolute_value=True
             )
 
-        def rec(r, q):
-            nc.vector.reciprocal(out=lnt[r][2][:, 2 * q : 2 * q + 2], in_=lnt[r][1][:, 2 * q : 2 * q + 2])
-
         def cast(r, b, on_vector):
             f8 = work.tile([P, D], FP8, name="f8", bufs=4)
             if on_vector:
@@ -478,7 +476,11 @@ def tile_coattention_pb_kernel(
 
         def casts(r, q):
             nc.scalar.activation(
-                out=lnt[r][3][:, 2 * q : 2 * q + 2], in_=lnt[r][2][:, 2 * q : 2 * q + 2], func=ACT.Copy, scale=448.0
+                out=lnt[r][2][:, 2 * q : 2 * q + 2], in_=lnt[r][1][:, 2 * q : 2 * q + 2], func=ACT.Abs_reciprocal_sqrt
+            )
+            nc.scalar.activation(
+                out=lnt[r][3][:, 2 * q : 2 * q + 2], in_=lnt[r][2][:, 2 * q : 2 * q + 2], func=ACT.Square,
+                scale=math.sqrt(448.0),
             )
             for b in (2 * q, 2 * q + 1):
                 cast(r, b, False)
@@ -497,8 +499,6 @@ def tile_coattention_pb_kernel(
                 act1(i + 1, (0,))
             if has(i):
                 stt1_v(i)
-            if has(i - 1):
-                rec(i - 1, 1)
             if has(i + 1):
                 ev(i + 1, 0, (0,))
                 act1(i + 1, (1, 2, 3))
@@ -514,8 +514,6 @@ def tile_coattention_pb_kernel(
             if has(i + 1):
                 tr(i + 1, 1, (0, 1, 2, 3))
                 ev(i + 1, 1, (0,))
-            if has(i):
-                rec(i, 0)
             if has(i + 1):
                 ev(i + 1, 1, (1, 2, 3))
                 total(i + 1)

import math
from contextlib import ExitStack

import concourse.mybir as mybir
from concourse.masks import make_identity

L, B, D = 512, 4, 1024
EPS_BN = 1e-5
EPS_LN = 1e-5
FLOPS = 2 * L * B * D * D

F32 = mybir.dt.float32
BF16 = mybir.dt.bfloat16
U32 = mybir.dt.uint32
U8 = mybir.dt.uint8
FP8X4 = mybir.dt.float8_e4m3fn_x4
FP8 = mybir.dt.float8_e4m3fn
ALU = mybir.AluOpType
ACT = mybir.ActivationFunctionType
AX = mybir.AxisListType

P = 128
NCT = D // P
HC = NCT // 2
HW = HC * P
NCH = L // P
CHUNK = B * P
NPASS = D // 512
ON_GPSIMD = ((0, 0), (0, 1))
NGS = (2, 3, 3, 3)
NSS = 1
HS = 6


def tile_coattention_pb_kernel(
    tc, x, res_a, ctx_v, W_v, bn_v_g, bn_v_b, prelu_v, ln_g, ln_b, out_0, out_1
):
    nc = tc.nc
    with ExitStack() as ctx:
        keep = ctx.enter_context(tc.tile_pool(name="keep", bufs=1))
        xin = ctx.enter_context(tc.tile_pool(name="xin", bufs=4))
        ypool = []

        ident = keep.tile([P, P], F32, name="ident")
        make_identity(nc, ident[:])
        one = keep.tile([P, 1], F32, name="one")
        nc.vector.memset(one[:], 1.0)
        zero = keep.tile([P, 1], F32, name="zero")
        nc.vector.memset(zero[:], 0.0)
        warm = keep.tile([P, 1], F32, name="warm")
        nc.scalar.activation(out=warm[:], in_=one[:], func=ACT.Abs_reciprocal_sqrt)

        w_codes = keep.tile([P, NPASS, D], U32, name="w_codes", align_bytes=64)
        w_scales = keep.tile([P, NPASS, D], U8, name="w_scales", align_bytes=64)
        c_codes = keep.tile([P, NPASS, NCH * CHUNK], U32, name="c_codes", align_bytes=64)
        c_scales = keep.tile([P, NPASS, NCH * CHUNK], U8, name="c_scales", align_bytes=64)
        bnst = keep.tile([P, NCT, NCH, 6], F32, name="bnst")
        ysave = keep.tile([P, HS, NCH * CHUNK], F32, name="ysave")
        o_t = [[keep.tile([P, D], F32, name="o_%d_%d" % (r, b)) for b in range(B)] for r in range(1)]
        g_sb = keep.tile([P, D], BF16, name="g_sb")
        ident_bf = keep.tile([P, P], BF16, name="ident_bf")
        sI_bf = keep.tile([P, P], BF16, name="sI_bf")
        lnT_bf = keep.tile([P, 2 * NCT], BF16, name="lnT_bf")
        a_bf = keep.tile([P, 1], BF16, name="a_bf")
        prm_bf = keep.tile([P, P], BF16, name="prm_bf")
        prm_f = keep.tile([P, P], F32, name="prm_f")
        sums = keep.tile([P, NCH, B, 2], F32, name="sums")
        a_f = keep.tile([P, 1], F32, name="a_f")
        sig = keep.tile([P, 1], F32, name="sig")
        k1 = keep.tile([P, 1], F32, name="k1")
        k2 = keep.tile([P, 1], F32, name="k2")
        mv = keep.tile([P, NCT, 2], F32, name="mv")
        sy = keep.tile([P, NSS, NCH], F32, name="sy")
        sq = keep.tile([P, NSS, NCH], F32, name="sq")
        negm0 = keep.tile([P, NSS], F32, name="negm0")
        toty = keep.tile([P, NSS], F32, name="toty")
        totq = keep.tile([P, NSS], F32, name="totq")
        dm = keep.tile([P, NSS], F32, name="dm")
        dm2 = keep.tile([P, NSS], F32, name="dm2")
        sjunk = keep.tile([P, CHUNK], BF16, name="sjunk")

        def mm(r, c):
            y = ypool[-1].tile([P, CHUNK], F32, name="y")
            for g in range(NPASS):
                nc.tensor.matmul_mx(
                    out=y[:],
                    lhsT=w_codes[:, g, c * P : (c + 1) * P].bitcast(FP8X4),
                    lhsT_scale=w_scales[:, g, c * P : (c + 1) * P],
                    rhs=c_codes[:, g, r * CHUNK : (r + 1) * CHUNK].bitcast(FP8X4),
                    rhs_scale=c_scales[:, g, r * CHUNK : (r + 1) * CHUNK],
                    start=(g == 0),
                    stop=(g == NPASS - 1),
                )
            return y

        x_raw = {}
        ra_raw = {}

        def load_xr(r, h):
            cols = slice(h * HW, (h + 1) * HW)
            x_raw[r, h] = xin.tile([P, B, HW], BF16, name="x_raw")
            nc.sync.dma_start(out=x_raw[r, h][:], in_=x[r * P : (r + 1) * P, :, cols])
            ra_raw[r, h] = xin.tile([P, B, HW], BF16, name="ra_raw")
            nc.sync.dma_start(
                out=ra_raw[r, h][:], in_=res_a[:, r * P : (r + 1) * P, cols].rearrange("b l d -> l b d")
            )

        def add_xr(r, h):
            for b in range(B):
                nc.gpsimd.tensor_tensor(
                    out=o_t[r][b][:, h * HW : (h + 1) * HW], in0=x_raw[r, h][:, b, :], in1=ra_raw[r, h][:, b, :],
                    op=ALU.add,
                )

        HALVES = (0, 1)
        gk = [keep.tile([P, NCT], F32, name="gk%d" % j) for j in (0, 1)]
        bk = [keep.tile([P, NCT], F32, name="bk%d" % j) for j in (0, 1)]
        brstd = [keep.tile([P, HC], F32, name="brstd%d" % h) for h in HALVES]
        psc = [[keep.tile([P, HC], F32, name="psc%d_%d" % (j, h)) for h in HALVES] for j in (0, 1)]
        pmn = [[keep.tile([P, HC], F32, name="pmn%d_%d" % (j, h)) for h in HALVES] for j in (0, 1)]
        pbi = [[keep.tile([P, HC], F32, name="pbi%d_%d" % (j, h)) for h in HALVES] for j in (0, 1)]
        s12 = {}
        ysrc = {}

        def chain(h):
            cs = slice(h * HC, (h + 1) * HC)
            nc.scalar.activation(out=brstd[h][:], in_=mv[:, cs, 1], func=ACT.Abs_reciprocal_sqrt, bias=EPS_BN, scale=1.0)
            for j in (1, 0):
                nc.vector.tensor_tensor(out=psc[j][h][:], in0=gk[j][:, cs], in1=brstd[h][:], op=ALU.mult)
            for j in (1, 0):
                nc.vector.tensor_tensor(out=pmn[j][h][:], in0=mv[:, cs, 0], in1=psc[j][h][:], op=ALU.mult)
            for j in (1, 0):
                nc.vector.tensor_tensor(out=pbi[j][h][:], in0=bk[j][:, cs], in1=pmn[j][h][:], op=ALU.subtract)

        def src_of(r, h, cc):
            c = h * HC + cc
            return ysave[:, c, r * CHUNK : (r + 1) * CHUNK] if c < HS else ysrc[r, cc][:]

        def new_block(r, h):
            s12[r, h] = work.tile([P, 2, HC, CHUNK], F32, name="s12")

        def s1(r, h, cc, eng):
            if eng == "S":
                nc.scalar.activation(
                    out=s12[r, h][:, 0, cc, :], in_=src_of(r, h, cc), func=ACT.Identity,
                    scale=psc[0][h][:, cc : cc + 1], bias=pbi[0][h][:, cc : cc + 1],
                )
            else:
                (nc.vector if eng == "V" else nc.gpsimd).tensor_scalar(
                    out=s12[r, h][:, 0, cc, :], in0=src_of(r, h, cc),
                    scalar1=psc[0][h][:, cc : cc + 1], scalar2=pbi[0][h][:, cc : cc + 1], op0=ALU.mult, op1=ALU.add,
                )

        def s2(r, h, cc):
            nc.scalar.activation(
                out=s12[r, h][:, 1, cc, :], in_=src_of(r, h, cc), func=ACT.Relu,
                scale=psc[1][h][:, cc : cc + 1], bias=pbi[1][h][:, cc : cc + 1],
            )

        def act0(r):
            new_block(r, 0)
            for cc in range(HC):
                s1(r, 0, cc, "G")
                s2(r, 0, cc)

        nc.vector.memset(prm_bf[:], 0.0)
        with tc.psum_pool(name="tpsum", bufs=3) as tpsum, tc.psum_pool(name="ypre", bufs=5) as ypre:
            ypool.append(ypre)

            def aggr(c):
                nc.vector.bn_aggr(out=mv[:, c, :], in_=bnst[:, c, :, :].rearrange("p r s -> p (r s)"))

            def square(r, c):
                nc.scalar.activation(
                    out=sjunk[:], in_=ysave[:, c, r * CHUNK : (r + 1) * CHUNK], func=ACT.Square,
                    bias=negm0[:, c : c + 1], scale=1.0, accum_out=sq[:, c, r : r + 1],
                )

            def scalar_stats():
                n_rows = NCH * CHUNK
                nc.vector.tensor_reduce(out=toty[:], in_=sy[:], axis=AX.X, op=ALU.add)
                nc.vector.tensor_reduce(out=totq[:], in_=sq[:], axis=AX.X, op=ALU.add)
                nc.vector.tensor_scalar(
                    out=mv[:, 0:NSS, 0], in0=toty[:], scalar1=1.0 / n_rows, scalar2=None, op0=ALU.mult
                )
                nc.vector.scalar_tensor_tensor(
                    out=dm[:], in0=toty[:], scalar=1.0 / n_rows, in1=negm0[:], op0=ALU.mult, op1=ALU.add
                )
                nc.vector.tensor_tensor(out=dm2[:], in0=dm[:], in1=dm[:], op=ALU.mult)
                nc.vector.scalar_tensor_tensor(
                    out=mv[:, 0:NSS, 1], in0=totq[:], scalar=1.0 / n_rows, in1=dm2[:], op0=ALU.mult, op1=ALU.subtract
                )

            def mm_stat(r, c):
                y = mm(r, c)
                if c < NSS:
                    nc.scalar.activation(
                        out=ysave[:, c, r * CHUNK : (r + 1) * CHUNK], in_=y[:], func=ACT.Copy,
                        accum_out=sy[:, c, r : r + 1],
                    )
                    if r > 0:
                        square(r, c)
                    elif c == NSS - 1:
                        nc.scalar.activation(out=negm0[:], in_=sy[:, :, 0], func=ACT.Copy, scale=-1.0 / CHUNK)
                        for c0 in range(NSS):
                            square(0, c0)
                    return
                nc.vector.bn_stats(out=bnst[:, c, r, :], in_=y[:])
                if c < HS:
                    nc.scalar.copy(out=ysave[:, c, r * CHUNK : (r + 1) * CHUNK], in_=y[:])
                if r == NCH - 1:
                    aggr(c)

            with tc.tile_pool(name="wstage", bufs=1) as wstage, tc.tile_pool(name="cstage", bufs=2) as cstage:
                w_raw = {}
                c_raw = {}
                w_grp = {}
                c_grp = {}

                def load_w(h, pieces):
                    w_raw[h] = wstage.tile([P, HC, D], BF16, name="w_raw", bufs=2)
                    n = HC // pieces
                    for q in range(pieces):
                        nc.sync.dma_start(
                            out=w_raw[h][:, n * q : n * (q + 1), :],
                            in_=W_v[(h * HC + n * q) * P : (h * HC + n * (q + 1)) * P, :].rearrange(
                                "(c p) k -> p c k", p=P
                            ),
                        )

                def load_ctx(r, pieces):
                    c_raw[r] = cstage.tile([P, B, D], BF16, name="c_raw", bufs=NCH)
                    n = B // pieces
                    for q in range(pieces):
                        nc.sync.dma_start(
                            out=c_raw[r][:, n * q : n * (q + 1), :],
                            in_=ctx_v[n * q : n * (q + 1), r * P : (r + 1) * P, :].rearrange("b l d -> l b d"),
                        )

                def grp_of(kind, j):
                    if kind == "W":
                        if j % HC == 0:
                            w_grp[j // HC] = wstage.tile([P, NPASS, HW, 4], BF16, name="w_grp", align_bytes=64)
                        return w_grp[j // HC]
                    if j % B == 0:
                        c_grp[j // B] = cstage.tile([P, NPASS, CHUNK, 4], BF16, name="c_grp", align_bytes=64)
                    return c_grp[j // B]

                def turn(kind, j, on_vector):
                    rows = w_raw[j // HC][:, j % HC, :] if kind == "W" else c_raw[j // B][:, j % B, :]
                    words = rows.bitcast(F32)
                    tp = tpsum.tile([P, NPASS, 2, P], F32, name="tp")
                    for g in range(NPASS):
                        for u in range(2):
                            nc.tensor.transpose(tp[:, g, u, :], words[:, 256 * g + u : 256 * (g + 1) : 2], ident[:])
                    grouped = grp_of(kind, j)[:, :, (j % 4) * P : (j % 4 + 1) * P, :]
                    if on_vector:
                        nc.vector.tensor_copy(out=grouped.bitcast(F32), in_=tp[:].rearrange("p g u r -> p g r u"))
                    else:
                        nc.scalar.copy(out=grouped.bitcast(F32), in_=tp[:].rearrange("p g u r -> p g r u"))

                def quant(kind, j, n):
                    codes, scales = (w_codes, w_scales) if kind == "W" else (c_codes, c_scales)
                    grp = w_grp[j // 4] if kind == "W" else c_grp[j // 4]
                    for g in range(NPASS):
                        nc.vector.quantize_mx(
                            out=codes[:, g, j * P : (j + n) * P].bitcast(FP8X4),
                            scales=scales[:, g, j * P : (j + n) * P],
                            in_=grp[:, g, (j % 4) * P : (j % 4 + n) * P, :].rearrange("p c t -> p (c t)"),
                        )

                load_ctx(0, 4)
                load_w(0, 4)
                load_w(1, 4)
                nc.sync.dma_start(out=prm_bf[0:NCT, :], in_=bn_v_g.rearrange("(c p) -> c p", p=P))
                nc.sync.dma_start(out=prm_bf[NCT : 2 * NCT, :], in_=bn_v_b.rearrange("(c p) -> c p", p=P))
                nc.sync.dma_start(out=prm_bf[2 * NCT : 3 * NCT, :], in_=ln_g.rearrange("(c p) -> c p", p=P))
                nc.sync.dma_start(out=prm_bf[3 * NCT : 4 * NCT, :], in_=ln_b.rearrange("(c p) -> c p", p=P))
                nc.sync.dma_start(out=a_bf[:], in_=prelu_v.partition_broadcast(P))
                for r in range(1, NCH):
                    load_ctx(r, 2)
                load_xr(0, 0)
                load_xr(0, 1)
                load_xr(1, 0)
                load_xr(1, 1)
                nc.sync.dma_start(out=g_sb[:], in_=ln_g.partition_broadcast(P))

                def unit(kind, j, mms):
                    turn(kind, j, False)
                    turn(kind, j + 1, False)
                    mm_stat(mms[0][0], mms[0][1])
                    quant(kind, j, 2)
                    for rc in mms[1:]:
                        mm_stat(rc[0], rc[1])

                for b in range(B):
                    turn("X", b, b % 2 == 1)
                    if b % 2 == 1:
                        quant("X", b - 1, 2)
                for c in range(2):
                    turn("W", c, False)
                    quant("W", c, 1)
                    mm_stat(0, c)
                for c in range(2, NCT, 2):
                    turn("W", c, False)
                    turn("W", c + 1, False)
                    quant("W", c, 2)
                    mm_stat(0, c)
                    mm_stat(0, c + 1)
                    if c >= HC:
                        turn("X", c, False)
                        turn("X", c + 1, False)
                        quant("X", c, 2)
                nc.gpsimd.tensor_copy(out=ident_bf[:], in_=ident[:])
                nc.gpsimd.tensor_copy(out=prm_f[:], in_=prm_bf[:])
                nc.gpsimd.tensor_copy(out=a_f[:], in_=a_bf[:])
                nc.gpsimd.tensor_scalar(out=sig[:], in0=a_f[:], scalar1=1.0, scalar2=-2.0, op0=ALU.is_gt, op1=ALU.mult)
                nc.gpsimd.tensor_scalar(out=sig[:], in0=sig[:], scalar1=1.0, scalar2=None, op0=ALU.add)
                nc.gpsimd.tensor_scalar(out=k1[:], in0=a_f[:], scalar1=1.0, scalar2=None, op0=ALU.min)
                nc.gpsimd.tensor_tensor(out=k1[:], in0=k1[:], in1=sig[:], op=ALU.mult)
                nc.gpsimd.tensor_scalar(out=k2[:], in0=a_f[:], scalar1=-1.0, scalar2=1.0, op0=ALU.mult, op1=ALU.add)
                nc.gpsimd.tensor_scalar(out=sI_bf[:], in0=ident[:], scalar1=sig[:, 0:1], scalar2=None, op0=ALU.mult)
                prmT = tpsum.tile([P, NPASS, 2, P], F32, name="tp")
                nc.tensor.transpose(prmT[:, 0, 0, :], prm_f[:], ident[:])
                nc.scalar.copy(out=lnT_bf[:], in_=prmT[:, 0, 0, 2 * NCT : 4 * NCT])
                for j in (0, 1):
                    kj = k1 if j == 0 else k2
                    nc.scalar.activation(out=gk[j][:], in_=prmT[:, 0, 0, 0:NCT], func=ACT.Copy, scale=kj[:, 0:1])
                    nc.scalar.activation(
                        out=bk[j][:], in_=prmT[:, 0, 0, NCT : 2 * NCT], func=ACT.Copy, scale=kj[:, 0:1]
                    )
                for r in range(1, NCH - 1):
                    unit("X", B * r + B, [(r, c) for c in range(HC)])
                    unit("X", B * r + B + 2, [(r, c) for c in range(HC, NCT)])
            work = ctx.enter_context(tc.tile_pool(name="work", bufs=2))
            for r in range(1, NCH):
                o_t.append([work.tile([P, D], F32, name="o_%d_%d" % (r, b), bufs=1) for b in range(B)])
            for c in range(HC):
                mm_stat(NCH - 1, c)
            scalar_stats()
            chain(0)
            act0(0)
            for c in range(HC, NCT):
                mm_stat(NCH - 1, c)
            chain(1)
            for rh in ON_GPSIMD:
                add_xr(rh[0], rh[1])

        gbpsum = ctx.enter_context(tc.psum_pool(name="gbpsum", bufs=1))
        g_ps = gbpsum.tile([P, D], BF16, name="g_ps")
        b_ps = gbpsum.tile([P, D], BF16, name="b_ps")
        for c in range(NCT):
            nc.tensor.transpose(g_ps[:, c * P : (c + 1) * P], lnT_bf[:, c : c + 1].to_broadcast([P, P]), ident_bf[:])
            nc.tensor.transpose(
                b_ps[:, c * P : (c + 1) * P], lnT_bf[:, NCT + c : NCT + c + 1].to_broadcast([P, P]), ident_bf[:]
            )

        ctx.enter_context(tc.manual_schedule())
        opsum = ctx.enter_context(tc.psum_pool(name="opsum", bufs=4))
        ypool.append(ctx.enter_context(tc.psum_pool(name="ypost", bufs=2)))
        negmu = {}
        stdv = {}
        t1 = {}
        lnt = {}

        def mm_f(r, ccs):
            for cc in ccs:
                if HC + cc >= HS:
                    ysrc[r, cc] = mm(r, HC + cc)

        def act1(r, ccs):
            for cc in ccs:
                s2(r, 1, cc)
                if HC + cc >= HS:
                    s1(r, 1, cc, "S")

        def act1_g(r):
            for cc in range(HS - HC):
                s1(r, 1, cc, "G")

        ots = {}

        def tr(r, h, bs):
            on_pe = (r, h) not in ON_GPSIMD
            for b in bs:
                ot = opsum.tile([P, HW], F32, name="ot")
                if on_pe:
                    nc.tensor.matmul(out=ot[:], lhsT=sI_bf[:], rhs=ra_raw[r, h][:, b, :], start=True, stop=False)
                for cc in range(HC):
                    for j in range(2):
                        nc.tensor.matmul(
                            out=ot[:, cc * P : (cc + 1) * P],
                            lhsT=s12[r, h][:, j, cc, b * P : (b + 1) * P],
                            rhs=ident[:],
                            is_transpose=True,
                            start=(j == 0 and not on_pe),
                            stop=(j == 1 and (cc == HC - 1 or not on_pe)),
                        )
                ots[r, h, b] = ot

        def ev(r, h, bs):
            on_pe = (r, h) not in ON_GPSIMD
            for b in bs:
                dst = o_t[r][b][:, h * HW : (h + 1) * HW]
                nc.vector.scalar_tensor_tensor(
                    out=dst, in0=ots[r, h, b][:], scalar=sig[:, 0:1], in1=(x_raw[r, h][:, b, :] if on_pe else dst),
                    op0=ALU.mult, op1=ALU.add, accum_out=sums[:, r, b, h : h + 1],
                )

        tots = {}

        def total(r):
            tots[r] = work.tile([P, B], F32, name="tot")
            nc.vector.tensor_reduce(out=tots[r][:], in_=sums[:, r, :, :], axis=AX.X, op=ALU.add)

        def stats(r):
            negmu[r] = work.tile([P, B], F32, name="negmu")
            nc.scalar.activation(out=negmu[r][:], in_=tots[r][:], func=ACT.Copy, scale=-1.0 / D)
            ssq = work.tile([P, B], F32, name="ssq")
            for b in range(B):
                junk = work.tile([P, D], BF16, name="junk", bufs=1)
                nc.scalar.activation(
                    out=junk[:], in_=o_t[r][b][:], func=ACT.Square,
                    bias=negmu[r][:, b : b + 1], scale=1.0, accum_out=ssq[:, b : b + 1],
                )
            stdv[r] = work.tile([P, B], F32, name="rstd")
            nc.scalar.activation(
                out=stdv[r][:], in_=ssq[:], func=ACT.Abs_reciprocal_sqrt, bias=EPS_LN, scale=1.0 / D
            )

        def stt1_g(r):
            for b in range(B - NGS[r], B):
                t1[r, b] = work.tile([P, D], F32, name="t1g", bufs=3)
                nc.gpsimd.tensor_scalar(
                    out=t1[r, b][:], in0=o_t[r][b][:], scalar1=negmu[r][:, b : b + 1], scalar2=1.0,
                    op0=ALU.add, op1=ALU.mult,
                )
                nc.gpsimd.tensor_tensor(out=t1[r, b][:], in0=t1[r, b][:], in1=g_sb[:], op=ALU.mult)

        def stt1_v(r):
            for b in range(B - NGS[r]):
                t1[r, b] = work.tile([P, D], F32, name="t1v", bufs=2)
                nc.vector.scalar_tensor_tensor(
                    out=t1[r, b][:], in0=o_t[r][b][:], scalar=negmu[r][:, b : b + 1], in1=g_ps[:],
                    op0=ALU.add, op1=ALU.mult,
                )

        def ln_open(r):
            lnt[r] = [stdv[r]] + [work.tile([P, B], F32, name=n) for n in ("amax", "ram", "r448")]

        def stt2(r, b):
            nc.vector.scalar_tensor_tensor(
                out=o_t[r][b][:], in0=t1[r, b][:], scalar=lnt[r][0][:, b : b + 1], in1=b_ps[:],
                op0=ALU.mult, op1=ALU.add,
            )
            nc.sync.dma_start(out=out_0[r * P : (r + 1) * P, b, :], in_=o_t[r][b][:])

        def amx(r, b):
            nc.vector.tensor_reduce(
                out=lnt[r][1][:, b : b + 1], in_=o_t[r][b][:], axis=AX.X, op=ALU.max, apply_absolute_value=True
            )

        def cast(r, b, on_vector):
            f8 = work.tile([P, D], FP8, name="f8", bufs=4)
            if on_vector:
                nc.vector.tensor_scalar(
                    out=f8[:], in0=o_t[r][b][:], scalar1=lnt[r][3][:, b : b + 1], scalar2=None, op0=ALU.mult,
                    saturate=False,
                )
            else:
                nc.scalar.activation(
                    out=f8[:], in_=o_t[r][b][:], func=ACT.Identity,
                    scale=lnt[r][3][:, b : b + 1], bias=zero[:, 0:1], saturate=False,
                )
            nc.sync.dma_start(out=out_1[r * P : (r + 1) * P, b, :], in_=f8[:].bitcast(U8))

        def casts(r, q):
            nc.scalar.activation(
                out=lnt[r][2][:, 2 * q : 2 * q + 2], in_=lnt[r][1][:, 2 * q : 2 * q + 2], func=ACT.Abs_reciprocal_sqrt
            )
            nc.scalar.activation(
                out=lnt[r][3][:, 2 * q : 2 * q + 2], in_=lnt[r][2][:, 2 * q : 2 * q + 2], func=ACT.Square,
                scale=math.sqrt(448.0),
            )
            for b in (2 * q, 2 * q + 1):
                cast(r, b, False)

        def ln_half(r, q):
            stt2(r, 2 * q)
            stt2(r, 2 * q + 1)
            amx(r, 2 * q)
            amx(r, 2 * q + 1)

        def has(r):
            return 0 <= r < NCH

        for i in range(-2, NCH):
            if has(i + 1):
                act1(i + 1, (0,))
            if has(i):
                stt1_v(i)
            if has(i + 1):
                ev(i + 1, 0, (0,))
                act1(i + 1, (1, 2, 3))
                ev(i + 1, 0, (1, 2))
            if has(i):
                ln_open(i)
            if has(i + 1):
                ev(i + 1, 0, (3,))
            if has(i - 1):
                casts(i - 1, 1)
            if has(i):
                ln_half(i, 0)
            if has(i + 1):
                tr(i + 1, 1, (0, 1, 2, 3))
                ev(i + 1, 1, (0,))
            if has(i + 1):
                ev(i + 1, 1, (1, 2, 3))
                total(i + 1)
                if has(i + 3):
                    load_xr(i + 3, 0)
                    load_xr(i + 3, 1)
            if has(i + 2) and i + 2 > 0:
                act0(i + 2)
            if has(i + 2):
                new_block(i + 2, 1)
                act1_g(i + 2)
            if has(i):
                casts(i, 0)
            if has(i + 1):
                stats(i + 1)
                stt1_g(i + 1)
            if has(i + 2):
                mm_f(i + 2, (0, 1, 2, 3))
                tr(i + 2, 0, (0, 1, 2, 3))
            if has(i) and i < NCH - 1:
                ln_half(i, 1)
        r = NCH - 1
        stt2(r, 2)
        stt2(r, 3)
        amx(r, 2)
        nc.vector.reciprocal(out=lnt[r][2][:, 2:3], in_=lnt[r][1][:, 2:3])
        amx(r, 3)
        nc.scalar.activation(out=lnt[r][3][:, 2:3], in_=lnt[r][2][:, 2:3], func=ACT.Copy, scale=448.0)
        cast(r, 2, False)
        nc.vector.reciprocal(out=lnt[r][2][:, 3:4], in_=lnt[r][1][:, 3:4])
        nc.vector.tensor_scalar(out=lnt[r][3][:, 3:4], in0=lnt[r][2][:, 3:4], scalar1=448.0, scalar2=None, op0=ALU.mult)
        cast(r, 3, True)
